import numpy as np
import ml_dtypes


def mxq(x, axis, fmt="e4m3"):
    dtype, down = {"e4m3": (ml_dtypes.float8_e4m3fn, 7), "e5m2": (ml_dtypes.float8_e5m2, 14)}[fmt]
    v = np.moveaxis(np.asarray(x, np.float32).astype(ml_dtypes.bfloat16).astype(np.float64), axis, -1)
    blocks = v.reshape(v.shape[:-1] + (-1, 32))
    amax = np.abs(blocks).max(-1, keepdims=True)
    byte = np.maximum(np.where(amax > 0, np.frexp(amax)[1] - 1 + 127, 0) - down, 1)
    scale = np.exp2(byte - 127.0)
    codes = (blocks / scale).astype(np.float32).astype(dtype).astype(np.float64)
    return np.moveaxis((codes * scale).reshape(v.shape), -1, axis)


WIDE = False


def mx_kscale(k):
    if not WIDE:
        return np.ones(k)
    levels = np.array([10, -10, 5, -5, 0])
    if k % 512:
        return np.exp2(np.random.permutation(np.resize(levels, k // 32))).repeat(32)
    a = np.empty((k // 512, 16))
    for p in range(k // 512):
        a[p, :8] = np.random.permutation(np.resize(levels, 8))
        for g in range(8):
            far = levels[np.abs(levels - a[p, g]) >= 10]
            a[p, g + 8] = far[np.random.randint(len(far))]
    return np.exp2(a.ravel()).repeat(32)


BF16 = ml_dtypes.bfloat16


def bf(x):
    return np.asarray(x, np.float32).astype(BF16)


def f64(x):
    return np.asarray(x).astype(np.float64)


N, C, O, OH, OW, KH, KW, STRIDE, PAD = 512, 128, 512, 3, 2, 3, 3, 1, 1
H, W = (OH - 1) * STRIDE + KH - 2 * PAD, (OW - 1) * STRIDE + KW - 2 * PAD
NEG_SLOPE = 0.1


def span(t, n_out, n_in):
    ok = [p for p in range(n_out) if 0 <= p * STRIDE + t - PAD < n_in]
    return ok[0], ok[-1] + 1


def preact(x, weight, bias):
    xf = f64(x)
    wt = f64(weight)[0]
    acc = np.zeros((N, O, OH, OW))
    for i in range(KH):
        h0, h1 = span(i, OH, H)
        a0 = h0 * STRIDE + i - PAD
        for j in range(KW):
            w0, w1 = span(j, OW, W)
            b0 = w0 * STRIDE + j - PAD
            xs = xf[:, :, a0:a0 + (h1 - h0 - 1) * STRIDE + 1:STRIDE, b0:b0 + (w1 - w0 - 1) * STRIDE + 1:STRIDE]
            ws = wt[:, :, h0:h1, w0:w1, i * KW + j]
            acc[:, :, h0:h1, w0:w1] += (xs.transpose(2, 3, 0, 1) @ ws.transpose(2, 3, 1, 0)).transpose(2, 3, 0, 1)
    return acc + f64(bias)


def setup_inputs():
    s = mx_kscale(N)
    u = mx_kscale(O)
    x0 = bf(np.random.standard_normal((N, C, H, W)))
    wt0 = bf(np.random.standard_normal((1, O, C, OH, OW, KH * KW)) * np.sqrt(2.0 / (KH * KW * C)))
    bias = bf(np.random.standard_normal((1, O, OH, OW)) * 0.3)
    g = bf(np.random.standard_normal((N, O, OH, OW)) * np.exp2(np.random.randint(-6, 1, (N, 1, OH, OW))) * 2.0
           / s[:, None, None, None] * u[None, :, None, None])
    z = preact(x0, wt0, bias)
    return {"x": bf(f64(x0) * s[:, None, None, None]),
            "weight": bf(f64(wt0) / u[None, :, None, None, None, None]),
            "bias": bias,
            "z": np.asarray(z, np.float32),
            "grad_out": g}


def reference(x, weight, bias, z, grad_out):
    dz = f64(grad_out) * np.where(f64(z) >= 0, 1.0, NEG_SLOPE)
    dqo = mxq(dz, 1, "e5m2")
    dqn = mxq(dz, 0, "e5m2")
    xq = mxq(f64(x), 0, "e4m3")
    wt = f64(weight)[0]
    gx = np.zeros((N, C, H, W))
    gw = np.zeros((O, C, OH, OW, KH * KW))
    for i in range(KH):
        h0, h1 = span(i, OH, H)
        a0 = h0 * STRIDE + i - PAD
        a1 = a0 + (h1 - h0 - 1) * STRIDE + 1
        for j in range(KW):
            w0, w1 = span(j, OW, W)
            b0 = w0 * STRIDE + j - PAD
            b1 = b0 + (w1 - w0 - 1) * STRIDE + 1
            k = i * KW + j
            ds = dqo[:, :, h0:h1, w0:w1]
            wq = mxq(wt[:, :, h0:h1, w0:w1, k], 0, "e4m3")
            p = ds.transpose(2, 3, 0, 1) @ wq.transpose(2, 3, 0, 1)
            gx[:, :, a0:a1:STRIDE, b0:b1:STRIDE] += p.transpose(2, 3, 0, 1)
            xs = xq[:, :, a0:a1:STRIDE, b0:b1:STRIDE]
            dn = dqn[:, :, h0:h1, w0:w1]
            q = xs.transpose(2, 3, 1, 0) @ dn.transpose(2, 3, 0, 1)
            gw[:, :, h0:h1, w0:w1, k] = q.transpose(3, 2, 0, 1)
    return gx, gw[None]

@@ -1,0 +1,325 @@
+from contextlib import ExitStack
+
+import concourse.mybir as mybir
+from concourse.masks import make_identity
+
+F32 = mybir.dt.float32
+BF16 = mybir.dt.bfloat16
+U32 = mybir.dt.uint32
+U8 = mybir.dt.uint8
+I32 = mybir.dt.int32
+E4M3 = mybir.dt.float8_e4m3fn_x4
+E5M2 = mybir.dt.float8_e5m2_x4
+ALU = mybir.AluOpType
+
+P = 128
+PLACES = 6
+ROW = 128 * 54
+HALF = ROW // 2
+FLOPS = 2 * 2 * 28 * 512 * 512 * 128
+BYTES = 512 * 768 * 2 + 28 * 512 * 128 * 2 + 512 * 3072 * 6 + 512 * 768 * 4 + 512 * ROW * 4
+
+W_BASE = (0, 512, 1024, 1792, 2560, 3328)
+
+SCHEDULE = (
+    ("ident",), ("Lz", 0), ("Lg", 0), ("Lx",), ("Lz", 1), ("Lg", 1), ("Z0", 0), ("Z0", 3), ("ZK",),
+    ("ZC", 1, "a"), ("ZC", 2, "a"), ("M", 0), ("T", 0), ("Lz", 2), ("Lg", 2), ("Lw", 0), ("XG", "a"),
+    ("GA", 0, "v"), ("XQ",), ("QA", 0), ("M", 1), ("T", 1), ("Lz", 3), ("Lg", 3), ("GA", 1, "v"), ("QA", 1),
+    ("U", 0, 0, "a"), ("Lw", 1), ("U", 0, 1, "a"), ("M", 2), ("T", 2), ("GA", 2, "v"), ("QA", 2),
+    ("U", 1, 0, "a"), ("U", 1, 1, "a"), ("M", 3), ("T", 3), ("GA", 3, "v"), ("QA", 3), ("BG", 0, "v"),
+    ("BG", 3, "a"), ("BG", 1, "v"), ("BG", 4, "a"), ("BQ", 0), ("BG", 2, "v"), ("BG", 5, "a"), ("BQ", 1),
+    ("BQ", 2), ("U", 2, 0, "a"), ("OO", (0, 1,)), ("WG", 0, "v"), ("WG", 1, "v"), ("WQ", 0),
+    ("OP", 0, (0, 1,)), ("US", 2, 1, 0, "a"), ("US", 2, 1, 1, "a"), ("US", 2, 1, 2, "a"), ("WG", 2, "v"),
+    ("WQ", 1), ("OP", 1, (0, 1,)), ("US", 2, 1, 3, "a"), ("US", 2, 1, 4, "a"), ("US", 2, 1, 5, "a"),
+    ("ST", 2, 1), ("BQ", 3), ("WG", 3, "v"), ("WQ", 2), ("OP", 2, (0, 1,)), ("US", 3, 0, 0, "a"),
+    ("US", 3, 0, 1, "a"), ("US", 3, 0, 2, "a"), ("BQ", 4), ("WG", 4, "v"), ("WQ", 3), ("OP", 3, (0, 1,)),
+    ("US", 3, 0, 3, "a"), ("US", 3, 0, 4, "a"), ("US", 3, 0, 5, "a"), ("ST", 3, 0), ("BQ", 5), ("WG", 5, "v"),
+    ("WQ", 4), ("OP", 4, (0, 1,)), ("US", 3, 1, 0, "a"), ("US", 3, 1, 1, "a"), ("US", 3, 1, 2, "a"),
+    ("WQ", 5), ("OP", 5, (0, 1,)), ("US", 3, 1, 3, "a"), ("US", 3, 1, 4, "a"), ("US", 3, 1, 5, "a"), ("OT",),
+    ("OE", 0, "v"), ("OO", (2,)), ("OP", 0, (2,)), ("OP", 1, (2,)), ("OP", 2, (2,)), ("OP", 3, (2,)),
+    ("OP", 4, (2,)), ("OP", 5, (2,)), ("OE", 1, "v"), ("ST", 3, 1), ("OO", (3,)), ("OP", 0, (3,)),
+    ("OP", 1, (3,)), ("OP", 2, (3,)), ("OP", 3, (3,)), ("OP", 4, (3,)), ("OP", 5, (3,)), ("OE", 2, "v"),
+    ("OE", 3, "v"),
+)
+
+
+def tile_locallyconnected2d_t_v_kernel(tc, x, weight, bias, z, grad_out, out_0, out_1):
+    nc = tc.nc
+    x_v = x.rearrange("(p j) c h w -> p j (c h w)", j=4)
+    z_v = z.rearrange("(p j) o h w -> p j (o h w)", j=4)
+    g_v = grad_out.rearrange("(p j) o h w -> p j (o h w)", j=4)
+    w_v = weight[0].rearrange("(p j) c h w k -> p j (c h w k)", j=4)
+    o0_v = out_0.rearrange("(p j) c h w -> p j (c h w)", j=4)
+    o1_v = out_1[0].rearrange("(b o) c h w k -> b o (c h w k)", b=4)
+
+    def copy_on(engine, out, in_):
+        if engine == "a":
+            nc.scalar.copy(out=out, in_=in_)
+        else:
+            nc.vector.tensor_copy(out=out, in_=in_)
+
+    with ExitStack() as ctx:
+        keep = ctx.enter_context(tc.tile_pool(name="keep", bufs=1))
+        rot = ctx.enter_context(tc.tile_pool(name="rot", bufs=2))
+        psum = ctx.enter_context(tc.psum_pool(name="psum", bufs=2))
+        ctx.enter_context(tc.manual_schedule())
+
+        ident = keep.tile([P, P], F32, name="ident")
+        xq = keep.tile([P, 1024], U32, name="xq", align_bytes=64)
+        xs = keep.tile([P, 1024], U8, name="xs", align_bytes=64)
+        d = keep.tile([P, 4, PLACES, 512], BF16, name="d", align_bytes=64)
+        wr = keep.tile([P, 4, ROW], BF16, name="wr", align_bytes=64)
+        wq = keep.tile([P, 4096], U32, name="wq", align_bytes=64)
+        ws = keep.tile([P, 4096], U8, name="ws", align_bytes=64)
+        bq = keep.tile([P, PLACES * 512], U32, name="bq", align_bytes=64)
+        bs = keep.tile([P, PLACES * 512], U8, name="bs", align_bytes=64)
+        o1_a = keep.tile([P, HALF], F32, name="o1_a", align_bytes=64)
+        o1_b = keep.tile([P, HALF], F32, name="o1_b", align_bytes=64)
+        o1_c = keep.tile([P, HALF], F32, name="o1_c", align_bytes=64)
+        o1_d = keep.tile([P, HALF], F32, name="o1_d", align_bytes=64)
+        o1_tiles = (o1_a, o1_b, o1_c, o1_d)
+        live = {}
+        xr = wr[:, 3, 0:3072].rearrange("p (j f) -> p j f", j=4)
+        xg = wr[:, 3, 3072:6144]
+
+        def load_x():
+            nc.sync.dma_start(out=xr, in_=x_v)
+
+        def load_z(b):
+            zb = rot.tile([P, 4, 768], F32, tag="z", name="zb", align_bytes=64)
+            nc.sync.dma_start(out=zb[:], in_=z_v[:, :, 768 * b : 768 * (b + 1)])
+            live["z", b] = zb
+
+        def load_g(b):
+            gb = rot.tile([P, 4, 768], BF16, tag="g", name="gb", align_bytes=64)
+            nc.sync.dma_start(out=gb[:], in_=g_v[:, :, 768 * b : 768 * (b + 1)])
+            live["g", b] = gb
+
+        def load_w(part):
+            nc.sync.dma_start(out=wr[:, 2 * part : 2 * part + 2, :], in_=w_v[:, 2 * part : 2 * part + 2, :])
+
+        def zero_first(n):
+            nc.vector.memset(o1_tiles[n][:], 0.0)
+
+        def zero_copy(n, engine):
+            copy_on(engine, o1_tiles[n][:], o1_a[:])
+
+        def zero_codes():
+            for hf in range(2):
+                nc.vector.memset(xq[:, 512 * hf + 384 : 512 * (hf + 1)].bitcast(I32), 0)
+                nc.vector.memset(xs[:, 512 * hf + 384 : 512 * (hf + 1)].bitcast(I32), 0)
+            for s in (4, 5):
+                nc.vector.memset(wq[:, W_BASE[s] : W_BASE[s] + 256].bitcast(I32), 0)
+                nc.vector.memset(ws[:, W_BASE[s] : W_BASE[s] + 256].bitcast(I32), 0)
+
+        def x_group(engine):
+            xr_v = xr.rearrange("p j (c h w) -> p h c w j", h=3, w=2)
+            for hf in range(2):
+                for h in range(3):
+                    copy_on(
+                        engine,
+                        xg[:, 1536 * hf + 512 * h : 1536 * hf + 512 * (h + 1)].rearrange(
+                            "p (c w j) -> p c w j", w=2, j=4
+                        ),
+                        xr_v[:, h, 64 * hf : 64 * (hf + 1)],
+                    )
+
+        def x_quant():
+            for hf in range(2):
+                nc.vector.quantize_mx(
+                    out=xq[:, 512 * hf : 512 * hf + 256].bitcast(E4M3),
+                    scales=xs[:, 512 * hf : 512 * hf + 256],
+                    in_=xg[:, 1536 * hf : 1536 * hf + 1024],
+                )
+                nc.vector.quantize_mx(
+                    out=xq[:, 512 * hf + 256 : 512 * hf + 384].bitcast(E4M3),
+                    scales=xs[:, 512 * hf + 256 : 512 * hf + 384],
+                    in_=xg[:, 1536 * hf + 1024 : 1536 * hf + 1536],
+                )
+
+        def slope(b):
+            zb = live["z", b]
+            nc.vector.tensor_scalar(
+                out=zb[:], in0=zb[:], scalar1=0.0, scalar2=0.1, op0=ALU.is_ge, op1=ALU.max
+            )
+
+        def dz(b):
+            nc.vector.tensor_tensor(
+                out=d[:, :, :, 128 * b : 128 * (b + 1)],
+                in0=live["z", b][:].rearrange("p j (o s) -> p j s o", s=PLACES),
+                in1=live["g", b][:].rearrange("p j (o s) -> p j s o", s=PLACES),
+                op=ALU.mult,
+            )
+
+        def a_group(b, engine):
+            ga = rot.tile([P, 3072], BF16, tag="ga", name="ga", align_bytes=64)
+            copy_on(
+                engine,
+                ga[:].rearrange("p (s o j) -> p s o j", s=PLACES, j=4),
+                d[:].rearrange("p j s o -> p s o j")[:, :, 128 * b : 128 * (b + 1), :],
+            )
+            live["ga", b] = ga
+
+        def a_quant(b):
+            ga = live["ga", b]
+            aq = rot.tile([P, 768], U32, tag="aq", name="aq", align_bytes=64, bufs=3)
+            asc = rot.tile([P, 768], U8, tag="asc", name="asc", align_bytes=64, bufs=3)
+            nc.vector.quantize_mx(out=aq[:, 0:512].bitcast(E5M2), scales=asc[:, 0:512], in_=ga[:, 0:2048])
+            nc.vector.quantize_mx(out=aq[:, 512:768].bitcast(E5M2), scales=asc[:, 512:768], in_=ga[:, 2048:3072])
+            live["aq", b] = (aq, asc)
+
+        def unit_place(b, hf, s, engine):
+            aq, asc = live["aq", b]
+            stage_v = o1_tiles[(2 * b + hf) % 4][:].rearrange("p (c r t) -> p c r t", r=18, t=3)
+            h, w = divmod(s, 2)
+            pt = psum.tile([P, 512], F32, tag="u", name="pt1", bufs=4)
+            nc.tensor.matmul_mx(
+                out=pt[:],
+                lhsT=aq[:, 128 * s : 128 * (s + 1)].bitcast(E5M2),
+                lhsT_scale=asc[:, 128 * s : 128 * (s + 1)],
+                rhs=xq[:, 512 * hf : 512 * (hf + 1)].bitcast(E4M3),
+                rhs_scale=xs[:, 512 * hf : 512 * (hf + 1)],
+                start=True,
+                stop=True,
+            )
+            lo, hi = max(0, h - 1), min(2, h + 1)
+            copy_on(
+                engine,
+                stage_v[:, :, 3 * s + lo - h + 1 : 3 * s + hi - h + 2, 1 - w : 3 - w],
+                pt[:].rearrange("p (h c w) -> p c h w", h=4, w=2)[:, :, lo : hi + 1, :],
+            )
+
+        def unit_store(b, hf):
+            nc.sync.dma_start(out=o1_v[b][:, HALF * hf : HALF * (hf + 1)], in_=o1_tiles[(2 * b + hf) % 4][:])
+
+        def unit(b, hf, engine):
+            for s in range(PLACES):
+                unit_place(b, hf, s, engine)
+            unit_store(b, hf)
+
+        wr_v = wr[:].rearrange("p j (c r t) -> p c r t j", r=18, t=3)
+
+        def w_group(s, engine):
+            h, w = divmod(s, 2)
+            lo, hi = max(0, h - 1), min(2, h + 1)
+            wg = rot.tile([P, 3072], BF16, tag="ga", name="wg", align_bytes=64)
+            for n in range(hi - lo + 1):
+                copy_on(
+                    engine,
+                    wg[:, 1024 * n : 1024 * (n + 1)].rearrange("p (c w j) -> p c w j", w=2, j=4),
+                    wr_v[:, :, 3 * s + lo - h + 1 + n, 1 - w : 3 - w, :],
+                )
+            live["wg", s] = wg
+
+        def w_quant(s):
+            h = s // 2
+            wg = live["wg", s]
+            first = W_BASE[s] + (256 if h == 2 else 0)
+            nc.vector.quantize_mx(
+                out=wq[:, first : first + 512].bitcast(E4M3), scales=ws[:, first : first + 512], in_=wg[:, 0:2048]
+            )
+            if h == 1:
+                nc.vector.quantize_mx(
+                    out=wq[:, first + 512 : first + 768].bitcast(E4M3),
+                    scales=ws[:, first + 512 : first + 768],
+                    in_=wg[:, 2048:3072],
+                )
+
+        d_words = d[:].bitcast(F32).rearrange("p j s (q u) -> p j s u q", u=2)
+
+        def b_group(s, engine):
+            if s % 3 == 0:
+                live["gt3", s // 3] = rot.tile([P, 3, 2048], BF16, tag="z", name="gt3", align_bytes=64)
+            gt = live["gt3", s // 3][:, s % 3, :]
+            gt_words = gt.bitcast(F32).rearrange("p (j n u) -> p j n u", j=4, u=2)
+            for jj in range(2):
+                pt = psum.tile([P, 512], F32, tag="t", name="ptt", bufs=4)
+                for jl in range(2):
+                    for u in range(2):
+                        col = 128 * (2 * jl + u)
+                        nc.tensor.transpose(pt[:, col : col + 128], d_words[:, 2 * jj + jl, s, u, :], ident[:])
+                copy_on(
+                    engine,
+                    gt_words[:, 2 * jj : 2 * jj + 2],
+                    pt[:].rearrange("p (j u n) -> p j n u", j=2, u=2),
+                )
+            live["gt", s] = gt
+
+        def b_quant(s):
+            nc.vector.quantize_mx(
+                out=bq[:, 512 * s : 512 * (s + 1)].bitcast(E5M2),
+                scales=bs[:, 512 * s : 512 * (s + 1)],
+                in_=live["gt", s],
+            )
+
+        def out0_tile():
+            o0 = rot.tile([P, 4, 768], F32, tag="z", name="o0", align_bytes=64)
+            live["o0"] = o0
+
+        def out0_open(js):
+            for j in js:
+                pa = psum.tile([P, 512], F32, tag="t", name="pa", bufs=4)
+                pb = psum.tile([P, 512], F32, tag="t", name="pb", bufs=4)
+                live["acc", j] = (pa, pb)
+
+        def out0_place(s, js):
+            for j in js:
+                pa, pb = live["acc", j]
+                col = 512 * s + 128 * j
+                nc.tensor.matmul_mx(
+                    out=pa[:],
+                    lhsT=bq[:, col : col + 128].bitcast(E5M2),
+                    lhsT_scale=bs[:, col : col + 128],
+                    rhs=wq[:, W_BASE[s] : W_BASE[s] + 512].bitcast(E4M3),
+                    rhs_scale=ws[:, W_BASE[s] : W_BASE[s] + 512],
+                    start=(s == 0),
+                    stop=(s == PLACES - 1),
+                )
+                if s >= 2:
+                    nc.tensor.matmul_mx(
+                        out=pb[:],
+                        lhsT=bq[:, col : col + 128].bitcast(E5M2),
+                        lhsT_scale=bs[:, col : col + 128],
+                        rhs=wq[:, W_BASE[s] + 256 : W_BASE[s] + 768].bitcast(E4M3),
+                        rhs_scale=ws[:, W_BASE[s] + 256 : W_BASE[s] + 768],
+                        start=(s == 2),
+                        stop=(s == PLACES - 1),
+                    )
+
+        def out0_leave(j, engine):
+            o0 = live["o0"]
+            pa, pb = live["acc", j]
+            o0_t = o0[:].rearrange("p j (c h w) -> p j c h w", h=3, w=2)
+            copy_on(engine, o0_t[:, j, :, 0:2, :], pa[:].rearrange("p (h c w) -> p c h w", h=2, w=2))
+            copy_on(engine, o0_t[:, j, :, 2, :], pb[:, 256:512].rearrange("p (c w) -> p c w", w=2))
+            nc.sync.dma_start(out=o0_v[:, j, :], in_=o0[:, j, :])
+
+        steps = {
+            "ident": lambda: make_identity(nc, ident[:]),
+            "Lx": load_x,
+            "Lz": load_z,
+            "Lg": load_g,
+            "Lw": load_w,
+            "Z0": zero_first,
+            "ZC": zero_copy,
+            "ZK": zero_codes,
+            "XG": x_group,
+            "XQ": x_quant,
+            "M": slope,
+            "T": dz,
+            "GA": a_group,
+            "QA": a_quant,
+            "U": unit,
+            "US": unit_place,
+            "ST": unit_store,
+            "WG": w_group,
+            "WQ": w_quant,
+            "BG": b_group,
+            "BQ": b_quant,
+            "OT": out0_tile,
+            "OO": out0_open,
+            "OP": out0_place,
+            "OE": out0_leave,
+        }
+        for step in SCHEDULE:
+            steps[step[0]](*step[1:])

@@ -22,9 +22,9 @@ BYTES = 512 * 768 * 2 + 28 * 512 * 128 * 2 + 512 * 3072 * 6 + 512 * 768 * 4 + 51
 W_BASE = (0, 512, 1024, 1792, 2560, 3328)
 
 SCHEDULE = (
-    ("ident",), ("Lz", 0), ("Lg", 0), ("Lx",), ("Lz", 1), ("Lg", 1), ("Z0", 0), ("Z0", 3), ("ZK",),
-    ("ZC", 1, "a"), ("ZC", 2, "a"), ("M", 0), ("T", 0), ("Lz", 2), ("Lg", 2), ("Lw", 0), ("XG", "a"),
-    ("GA", 0, "v"), ("XQ",), ("QA", 0), ("M", 1), ("T", 1), ("Lz", 3), ("Lg", 3), ("GA", 1, "v"), ("QA", 1),
+    ("ident",), ("Lx",), ("Lz", 0), ("Lg", 0), ("Lz", 1), ("Lg", 1), ("Z0", 0), ("ZK",), ("ZC", 1, "a"),
+    ("ZC", 2, "a"), ("ZC", 3, "a"), ("XG", "v"), ("XQ",), ("M", 0), ("T", 0), ("Lz", 2), ("Lg", 2), ("Lw", 0),
+    ("GA", 0, "v"), ("QA", 0), ("M", 1), ("T", 1), ("Lz", 3), ("Lg", 3), ("GA", 1, "v"), ("QA", 1),
     ("U", 0, 0, "a"), ("Lw", 1), ("U", 0, 1, "a"), ("M", 2), ("T", 2), ("GA", 2, "v"), ("QA", 2),
     ("U", 1, 0, "a"), ("U", 1, 1, "a"), ("M", 3), ("T", 3), ("GA", 3, "v"), ("QA", 3), ("BG", 0, "v"),
     ("BG", 3, "a"), ("BG", 1, "v"), ("BG", 4, "a"), ("BQ", 0), ("BG", 2, "v"), ("BG", 5, "a"), ("BQ", 1),
@@ -67,7 +67,7 @@ def tile_locallyconnected2d_t_v_kernel(tc, x, weight, bias, z, grad_out, out_0, 
         ident = keep.tile([P, P], F32, name="ident")
         xq = keep.tile([P, 1024], U32, name="xq", align_bytes=64)
         xs = keep.tile([P, 1024], U8, name="xs", align_bytes=64)
-        d = keep.tile([P, 4, PLACES, 512], BF16, name="d", align_bytes=64)
+        d = keep.tile([P, 4, 128, PLACES, 4], BF16, name="d", align_bytes=64)
         wr = keep.tile([P, 4, ROW], BF16, name="wr", align_bytes=64)
         wq = keep.tile([P, 4096], U32, name="wq", align_bytes=64)
         ws = keep.tile([P, 4096], U8, name="ws", align_bytes=64)
@@ -145,9 +145,9 @@ def tile_locallyconnected2d_t_v_kernel(tc, x, weight, bias, z, grad_out, out_0, 
 
         def dz(b):
             nc.vector.tensor_tensor(
-                out=d[:, :, :, 128 * b : 128 * (b + 1)],
-                in0=live["z", b][:].rearrange("p j (o s) -> p j s o", s=PLACES),
-                in1=live["g", b][:].rearrange("p j (o s) -> p j s o", s=PLACES),
+                out=d[:, :, 32 * b : 32 * (b + 1)],
+                in0=live["z", b][:].rearrange("p j (q t s) -> p j q s t", t=4, s=PLACES),
+                in1=live["g", b][:].rearrange("p j (q t s) -> p j q s t", t=4, s=PLACES),
                 op=ALU.mult,
             )
 
@@ -155,8 +155,8 @@ def tile_locallyconnected2d_t_v_kernel(tc, x, weight, bias, z, grad_out, out_0, 
             ga = rot.tile([P, 3072], BF16, tag="ga", name="ga", align_bytes=64)
             copy_on(
                 engine,
-                ga[:].rearrange("p (s o j) -> p s o j", s=PLACES, j=4),
-                d[:].rearrange("p j s o -> p s o j")[:, :, 128 * b : 128 * (b + 1), :],
+                ga[:].rearrange("p (s q t j) -> p q s t j", s=PLACES, t=4, j=4),
+                d[:, :, 32 * b : 32 * (b + 1)].rearrange("p j q s t -> p q s t j"),
             )
             live["ga", b] = ga
 
@@ -225,7 +225,7 @@ def tile_locallyconnected2d_t_v_kernel(tc, x, weight, bias, z, grad_out, out_0, 
                     in_=wg[:, 2048:3072],
                 )
 
-        d_words = d[:].bitcast(F32).rearrange("p j s (q u) -> p j s u q", u=2)
+        d_words = d[:].bitcast(F32).rearrange("p j q s u -> p j s u q")
 
         def b_group(s, engine):
             if s % 3 == 0:

@@ -13,47 +13,36 @@ E5M2 = mybir.dt.float8_e5m2_x4
 ALU = mybir.AluOpType
 
 P = 128
+PACK = 4
 PLACES = 6
-ROW = 128 * 54
-HALF = ROW // 2
+BLOCKS = 4
+ROW = 128 * PLACES * 9
+HALF_ROW = ROW // 2
+CHUNK = 128 * PLACES
+X_ROW = 128 * PLACES
+W_WINDOW = 384
+NEG_SLOPE = 0.1
+
 FLOPS = 2 * 2 * 28 * 512 * 512 * 128
-BYTES = 512 * 768 * 2 + 28 * 512 * 128 * 2 + 512 * 3072 * 6 + 512 * 768 * 4 + 512 * ROW * 4
+BYTES = 2 * 512 * X_ROW + 2 * 28 * 512 * 128 + (4 + 2) * 512 * 512 * PLACES + 4 * 512 * X_ROW + 4 * 512 * ROW
 
-W_BASE = (0, 512, 1024, 1792, 2560, 3328)
 
-SCHEDULE = (
-    ("ident",), ("Lx",), ("Lz", 0), ("Lg", 0), ("Lz", 1), ("Lg", 1), ("Z0", 0), ("ZK",), ("ZC", 1, "a"),
-    ("ZC", 2, "a"), ("ZC", 3, "a"), ("XG", "v"), ("XQ",), ("M", 0), ("T", 0), ("Lz", 2), ("Lg", 2), ("Lw", 0),
-    ("GA", 0, "v"), ("QA", 0), ("M", 1), ("T", 1), ("Lz", 3), ("Lg", 3), ("GA", 1, "v"), ("QA", 1),
-    ("U", 0, 0, "a"), ("Lw", 1), ("U", 0, 1, "a"), ("M", 2), ("T", 2), ("GA", 2, "v"), ("QA", 2),
-    ("U", 1, 0, "a"), ("U", 1, 1, "a"), ("M", 3), ("T", 3), ("GA", 3, "v"), ("QA", 3), ("BG", 0, "v"),
-    ("BG", 3, "a"), ("BG", 1, "v"), ("BG", 4, "a"), ("BQ", 0), ("BG", 2, "v"), ("BG", 5, "a"), ("BQ", 1),
-    ("BQ", 2), ("U", 2, 0, "a"), ("OO", (0, 1,)), ("WG", 0, "v"), ("WG", 1, "v"), ("WQ", 0),
-    ("OP", 0, (0, 1,)), ("US", 2, 1, 0, "a"), ("US", 2, 1, 1, "a"), ("US", 2, 1, 2, "a"), ("WG", 2, "v"),
-    ("WQ", 1), ("OP", 1, (0, 1,)), ("US", 2, 1, 3, "a"), ("US", 2, 1, 4, "a"), ("US", 2, 1, 5, "a"),
-    ("ST", 2, 1), ("BQ", 3), ("WG", 3, "v"), ("WQ", 2), ("OP", 2, (0, 1,)), ("US", 3, 0, 0, "a"),
-    ("US", 3, 0, 1, "a"), ("US", 3, 0, 2, "a"), ("BQ", 4), ("WG", 4, "v"), ("WQ", 3), ("OP", 3, (0, 1,)),
-    ("US", 3, 0, 3, "a"), ("US", 3, 0, 4, "a"), ("US", 3, 0, 5, "a"), ("ST", 3, 0), ("BQ", 5), ("WG", 5, "v"),
-    ("WQ", 4), ("OP", 4, (0, 1,)), ("US", 3, 1, 0, "a"), ("US", 3, 1, 1, "a"), ("US", 3, 1, 2, "a"),
-    ("WQ", 5), ("OP", 5, (0, 1,)), ("US", 3, 1, 3, "a"), ("US", 3, 1, 4, "a"), ("US", 3, 1, 5, "a"), ("OT",),
-    ("OE", 0, "v"), ("OO", (2,)), ("OP", 0, (2,)), ("OP", 1, (2,)), ("OP", 2, (2,)), ("OP", 3, (2,)),
-    ("OP", 4, (2,)), ("OP", 5, (2,)), ("OE", 1, "v"), ("ST", 3, 1), ("OO", (3,)), ("OP", 0, (3,)),
-    ("OP", 1, (3,)), ("OP", 2, (3,)), ("OP", 3, (3,)), ("OP", 4, (3,)), ("OP", 5, (3,)), ("OE", 2, "v"),
-    ("OE", 3, "v"),
-)
+def x_rows(h):
+    return max(0, h - 1), min(2, h + 1)
 
 
 def tile_locallyconnected2d_t_v_kernel(tc, x, weight, bias, z, grad_out, out_0, out_1):
     nc = tc.nc
-    x_v = x.rearrange("(p j) c h w -> p j (c h w)", j=4)
-    z_v = z.rearrange("(p j) o h w -> p j (o h w)", j=4)
-    g_v = grad_out.rearrange("(p j) o h w -> p j (o h w)", j=4)
-    w_v = weight[0].rearrange("(p j) c h w k -> p j (c h w k)", j=4)
-    o0_v = out_0.rearrange("(p j) c h w -> p j (c h w)", j=4)
-    o1_v = out_1[0].rearrange("(b o) c h w k -> b o (c h w k)", b=4)
+
+    x_hbm = x.rearrange("(p slot) c h w -> p slot (c h w)", slot=PACK)
+    z_hbm = z.rearrange("(p slot) o h w -> p slot (o h w)", slot=PACK)
+    g_hbm = grad_out.rearrange("(p slot) o h w -> p slot (o h w)", slot=PACK)
+    w_hbm = weight[0].rearrange("(p t) c h w k -> p t (c h w k)", t=PACK)
+    out0_hbm = out_0.rearrange("(p slot) c h w -> p slot (c h w)", slot=PACK)
+    out1_hbm = out_1[0].rearrange("(blk o) c h w k -> blk o (c h w k)", blk=BLOCKS)
 
     def copy_on(engine, out, in_):
-        if engine == "a":
+        if engine == "scalar":
             nc.scalar.copy(out=out, in_=in_)
         else:
             nc.vector.tensor_copy(out=out, in_=in_)
@@ -61,265 +50,292 @@ def tile_locallyconnected2d_t_v_kernel(tc, x, weight, bias, z, grad_out, out_0, 
     with ExitStack() as ctx:
         keep = ctx.enter_context(tc.tile_pool(name="keep", bufs=1))
         rot = ctx.enter_context(tc.tile_pool(name="rot", bufs=2))
-        psum = ctx.enter_context(tc.psum_pool(name="psum", bufs=2))
+        psum = ctx.enter_context(tc.psum_pool(name="psum", bufs=4))
         ctx.enter_context(tc.manual_schedule())
 
         ident = keep.tile([P, P], F32, name="ident")
-        xq = keep.tile([P, 1024], U32, name="xq", align_bytes=64)
-        xs = keep.tile([P, 1024], U8, name="xs", align_bytes=64)
-        d = keep.tile([P, 4, 128, PLACES, 4], BF16, name="d", align_bytes=64)
-        wr = keep.tile([P, 4, ROW], BF16, name="wr", align_bytes=64)
-        wq = keep.tile([P, 4096], U32, name="wq", align_bytes=64)
-        ws = keep.tile([P, 4096], U8, name="ws", align_bytes=64)
-        bq = keep.tile([P, PLACES * 512], U32, name="bq", align_bytes=64)
-        bs = keep.tile([P, PLACES * 512], U8, name="bs", align_bytes=64)
-        o1_a = keep.tile([P, HALF], F32, name="o1_a", align_bytes=64)
-        o1_b = keep.tile([P, HALF], F32, name="o1_b", align_bytes=64)
-        o1_c = keep.tile([P, HALF], F32, name="o1_c", align_bytes=64)
-        o1_d = keep.tile([P, HALF], F32, name="o1_d", align_bytes=64)
-        o1_tiles = (o1_a, o1_b, o1_c, o1_d)
+        x_codes = keep.tile([P, 2 * 512], U32, name="x_codes", align_bytes=64)
+        x_scales = keep.tile([P, 2 * 512], U8, name="x_scales", align_bytes=64)
+        dz = keep.tile([P, PACK, 128, PLACES, PACK], BF16, name="dz", align_bytes=64)
+        w_raw = keep.tile([P, PACK, ROW], BF16, name="w_raw", align_bytes=64)
+        w_codes = keep.tile([P, 12 * W_WINDOW + 128], U32, name="w_codes", align_bytes=64)
+        w_scales = keep.tile([P, 12 * W_WINDOW + 128], U8, name="w_scales", align_bytes=64)
+        dzo_codes = keep.tile([P, PLACES * 512], U32, name="dzo_codes", align_bytes=64)
+        dzo_scales = keep.tile([P, PLACES * 512], U8, name="dzo_scales", align_bytes=64)
+        stage_0 = keep.tile([P, HALF_ROW], F32, name="stage_0", align_bytes=64)
+        stage_1 = keep.tile([P, HALF_ROW], F32, name="stage_1", align_bytes=64)
+        stage_2 = keep.tile([P, HALF_ROW], F32, name="stage_2", align_bytes=64)
+        stage_3 = keep.tile([P, HALF_ROW], F32, name="stage_3", align_bytes=64)
+        stages = (stage_0, stage_1, stage_2, stage_3)
+        x_raw = w_raw[:, 3, 0:3072].rearrange("p (slot f) -> p slot f", slot=PACK)
+        x_grouped = w_raw[:, 3, 3072:6144]
         live = {}
-        xr = wr[:, 3, 0:3072].rearrange("p (j f) -> p j f", j=4)
-        xg = wr[:, 3, 3072:6144]
 
         def load_x():
-            nc.sync.dma_start(out=xr, in_=x_v)
+            nc.sync.dma_start(out=x_raw, in_=x_hbm)
 
-        def load_z(b):
-            zb = rot.tile([P, 4, 768], F32, tag="z", name="zb", align_bytes=64)
-            nc.sync.dma_start(out=zb[:], in_=z_v[:, :, 768 * b : 768 * (b + 1)])
-            live["z", b] = zb
+        def load_z(blk):
+            z_sb = rot.tile([P, PACK, CHUNK], F32, tag="z", name="z_sb", align_bytes=64)
+            nc.sync.dma_start(out=z_sb[:], in_=z_hbm[:, :, CHUNK * blk : CHUNK * (blk + 1)])
+            live["z", blk] = z_sb
 
-        def load_g(b):
-            gb = rot.tile([P, 4, 768], BF16, tag="g", name="gb", align_bytes=64)
-            nc.sync.dma_start(out=gb[:], in_=g_v[:, :, 768 * b : 768 * (b + 1)])
-            live["g", b] = gb
+        def load_g(blk):
+            g_sb = rot.tile([P, PACK, CHUNK], BF16, tag="g", name="g_sb", align_bytes=64)
+            nc.sync.dma_start(out=g_sb[:], in_=g_hbm[:, :, CHUNK * blk : CHUNK * (blk + 1)])
+            live["g", blk] = g_sb
 
-        def load_w(part):
-            nc.sync.dma_start(out=wr[:, 2 * part : 2 * part + 2, :], in_=w_v[:, 2 * part : 2 * part + 2, :])
+        def load_w(half):
+            cols = slice(HALF_ROW * half, HALF_ROW * (half + 1))
+            nc.sync.dma_start(out=w_raw[:, :, cols], in_=w_hbm[:, :, cols])
 
-        def zero_first(n):
-            nc.vector.memset(o1_tiles[n][:], 0.0)
+        def zero_x_codes():
+            nc.vector.memset(x_codes[:].bitcast(I32), 0)
+            nc.vector.memset(x_scales[:].bitcast(I32), 0)
 
-        def zero_copy(n, engine):
-            copy_on(engine, o1_tiles[n][:], o1_a[:])
+        def zero_w_codes():
+            starts = [W_WINDOW * v + 256 for v in range(4)] + [W_WINDOW * v for v in range(8, 13)]
+            for first in starts:
+                nc.gpsimd.memset(w_codes[:, first : first + 128].bitcast(F32), 0.0)
+                nc.gpsimd.memset(w_scales[:, first : first + 128], 0)
 
-        def zero_codes():
-            for hf in range(2):
-                nc.vector.memset(xq[:, 512 * hf + 384 : 512 * (hf + 1)].bitcast(I32), 0)
-                nc.vector.memset(xs[:, 512 * hf + 384 : 512 * (hf + 1)].bitcast(I32), 0)
-            for s in (4, 5):
-                nc.vector.memset(wq[:, W_BASE[s] : W_BASE[s] + 256].bitcast(I32), 0)
-                nc.vector.memset(ws[:, W_BASE[s] : W_BASE[s] + 256].bitcast(I32), 0)
+        def zero_first_stage():
+            nc.vector.memset(stage_0[:], 0.0)
 
-        def x_group(engine):
-            xr_v = xr.rearrange("p j (c h w) -> p h c w j", h=3, w=2)
-            for hf in range(2):
-                for h in range(3):
-                    copy_on(
-                        engine,
-                        xg[:, 1536 * hf + 512 * h : 1536 * hf + 512 * (h + 1)].rearrange(
-                            "p (c w j) -> p c w j", w=2, j=4
-                        ),
-                        xr_v[:, h, 64 * hf : 64 * (hf + 1)],
+        def zero_other_stages():
+            for stage in stages[1:]:
+                nc.scalar.copy(out=stage[:], in_=stage_0[:])
+
+        def group_x():
+            src = x_raw.rearrange("p slot (c h w) -> p h c w slot", h=3, w=2)
+            for half in range(2):
+                for xrow in range(3):
+                    first = 1536 * half + 512 * xrow
+                    nc.vector.tensor_copy(
+                        out=x_grouped[:, first : first + 512].rearrange("p (c w slot) -> p c w slot", w=2, slot=PACK),
+                        in_=src[:, xrow, 64 * half : 64 * (half + 1)],
                     )
 
-        def x_quant():
-            for hf in range(2):
-                nc.vector.quantize_mx(
-                    out=xq[:, 512 * hf : 512 * hf + 256].bitcast(E4M3),
-                    scales=xs[:, 512 * hf : 512 * hf + 256],
-                    in_=xg[:, 1536 * hf : 1536 * hf + 1024],
-                )
-                nc.vector.quantize_mx(
-                    out=xq[:, 512 * hf + 256 : 512 * hf + 384].bitcast(E4M3),
-                    scales=xs[:, 512 * hf + 256 : 512 * hf + 384],
-                    in_=xg[:, 1536 * hf + 1024 : 1536 * hf + 1536],
-                )
+        def quantize_x():
+            for half in range(2):
+                for first, width in ((0, 256), (256, 128)):
+                    cols = slice(512 * half + first, 512 * half + first + width)
+                    nc.vector.quantize_mx(
+                        out=x_codes[:, cols].bitcast(E4M3),
+                        scales=x_scales[:, cols],
+                        in_=x_grouped[:, 1536 * half + PACK * first : 1536 * half + PACK * (first + width)],
+                    )
 
-        def slope(b):
-            zb = live["z", b]
+        def slope(blk):
+            z_sb = live["z", blk]
             nc.vector.tensor_scalar(
-                out=zb[:], in0=zb[:], scalar1=0.0, scalar2=0.1, op0=ALU.is_ge, op1=ALU.max
+                out=z_sb[:], in0=z_sb[:], scalar1=0.0, scalar2=NEG_SLOPE, op0=ALU.is_ge, op1=ALU.max
             )
 
-        def dz(b):
+        def multiply(blk):
             nc.vector.tensor_tensor(
-                out=d[:, :, 32 * b : 32 * (b + 1)],
-                in0=live["z", b][:].rearrange("p j (q t s) -> p j q s t", t=4, s=PLACES),
-                in1=live["g", b][:].rearrange("p j (q t s) -> p j q s t", t=4, s=PLACES),
+                out=dz[:, :, 32 * blk : 32 * (blk + 1)],
+                in0=live["z", blk][:].rearrange("p slot (q t s) -> p slot q s t", t=PACK, s=PLACES),
+                in1=live["g", blk][:].rearrange("p slot (q t s) -> p slot q s t", t=PACK, s=PLACES),
                 op=ALU.mult,
             )
 
-        def a_group(b, engine):
-            ga = rot.tile([P, 3072], BF16, tag="ga", name="ga", align_bytes=64)
-            copy_on(
-                engine,
-                ga[:].rearrange("p (s q t j) -> p q s t j", s=PLACES, t=4, j=4),
-                d[:, :, 32 * b : 32 * (b + 1)].rearrange("p j q s t -> p q s t j"),
+        def group_samples(blk):
+            grouped = rot.tile([P, PACK * CHUNK], BF16, tag="grouped", name="dzn_grouped", align_bytes=64)
+            nc.vector.tensor_copy(
+                out=grouped[:].rearrange("p (s q t slot) -> p q s t slot", s=PLACES, t=PACK, slot=PACK),
+                in_=dz[:, :, 32 * blk : 32 * (blk + 1)].rearrange("p slot q s t -> p q s t slot"),
             )
-            live["ga", b] = ga
+            live["dzn_grouped", blk] = grouped
 
-        def a_quant(b):
-            ga = live["ga", b]
-            aq = rot.tile([P, 768], U32, tag="aq", name="aq", align_bytes=64, bufs=3)
-            asc = rot.tile([P, 768], U8, tag="asc", name="asc", align_bytes=64, bufs=3)
-            nc.vector.quantize_mx(out=aq[:, 0:512].bitcast(E5M2), scales=asc[:, 0:512], in_=ga[:, 0:2048])
-            nc.vector.quantize_mx(out=aq[:, 512:768].bitcast(E5M2), scales=asc[:, 512:768], in_=ga[:, 2048:3072])
-            live["aq", b] = (aq, asc)
+        def quantize_samples(blk):
+            grouped = live["dzn_grouped", blk]
+            codes = rot.tile([P, CHUNK], U32, tag="dzn_codes", name="dzn_codes", align_bytes=64)
+            scales = rot.tile([P, CHUNK], U8, tag="dzn_scales", name="dzn_scales", align_bytes=64)
+            for first, width in ((0, 512), (512, 256)):
+                nc.vector.quantize_mx(
+                    out=codes[:, first : first + width].bitcast(E5M2),
+                    scales=scales[:, first : first + width],
+                    in_=grouped[:, PACK * first : PACK * (first + width)],
+                )
+            live["dzn", blk] = (codes, scales)
 
-        def unit_place(b, hf, s, engine):
-            aq, asc = live["aq", b]
-            stage_v = o1_tiles[(2 * b + hf) % 4][:].rearrange("p (c r t) -> p c r t", r=18, t=3)
-            h, w = divmod(s, 2)
-            pt = psum.tile([P, 512], F32, tag="u", name="pt1", bufs=4)
+        def out1_place(blk, half, place):
+            codes, scales = live["dzn", blk]
+            h, w = divmod(place, 2)
+            product = psum.tile([P, 512], F32, tag="out1", name="product")
             nc.tensor.matmul_mx(
-                out=pt[:],
-                lhsT=aq[:, 128 * s : 128 * (s + 1)].bitcast(E5M2),
-                lhsT_scale=asc[:, 128 * s : 128 * (s + 1)],
-                rhs=xq[:, 512 * hf : 512 * (hf + 1)].bitcast(E4M3),
-                rhs_scale=xs[:, 512 * hf : 512 * (hf + 1)],
+                out=product[:],
+                lhsT=codes[:, 128 * place : 128 * (place + 1)].bitcast(E5M2),
+                lhsT_scale=scales[:, 128 * place : 128 * (place + 1)],
+                rhs=x_codes[:, 512 * half : 512 * (half + 1)].bitcast(E4M3),
+                rhs_scale=x_scales[:, 512 * half : 512 * (half + 1)],
                 start=True,
                 stop=True,
             )
-            lo, hi = max(0, h - 1), min(2, h + 1)
-            copy_on(
-                engine,
-                stage_v[:, :, 3 * s + lo - h + 1 : 3 * s + hi - h + 2, 1 - w : 3 - w],
-                pt[:].rearrange("p (h c w) -> p c h w", h=4, w=2)[:, :, lo : hi + 1, :],
+            first, last = x_rows(h)
+            stage = stages[(2 * blk + half) % 4][:].rearrange("p (c r j) -> p c r j", r=3 * PLACES, j=3)
+            nc.scalar.copy(
+                out=stage[:, :, 3 * place + first - h + 1 : 3 * place + last - h + 2, 1 - w : 3 - w],
+                in_=product[:].rearrange("p (xrow c xcol) -> p c xrow xcol", xrow=4, xcol=2)[:, :, first : last + 1, :],
             )
 
-        def unit_store(b, hf):
-            nc.sync.dma_start(out=o1_v[b][:, HALF * hf : HALF * (hf + 1)], in_=o1_tiles[(2 * b + hf) % 4][:])
-
-        def unit(b, hf, engine):
-            for s in range(PLACES):
-                unit_place(b, hf, s, engine)
-            unit_store(b, hf)
-
-        wr_v = wr[:].rearrange("p j (c r t) -> p c r t j", r=18, t=3)
-
-        def w_group(s, engine):
-            h, w = divmod(s, 2)
-            lo, hi = max(0, h - 1), min(2, h + 1)
-            wg = rot.tile([P, 3072], BF16, tag="ga", name="wg", align_bytes=64)
-            for n in range(hi - lo + 1):
-                copy_on(
-                    engine,
-                    wg[:, 1024 * n : 1024 * (n + 1)].rearrange("p (c w j) -> p c w j", w=2, j=4),
-                    wr_v[:, :, 3 * s + lo - h + 1 + n, 1 - w : 3 - w, :],
-                )
-            live["wg", s] = wg
-
-        def w_quant(s):
-            h = s // 2
-            wg = live["wg", s]
-            first = W_BASE[s] + (256 if h == 2 else 0)
-            nc.vector.quantize_mx(
-                out=wq[:, first : first + 512].bitcast(E4M3), scales=ws[:, first : first + 512], in_=wg[:, 0:2048]
-            )
-            if h == 1:
-                nc.vector.quantize_mx(
-                    out=wq[:, first + 512 : first + 768].bitcast(E4M3),
-                    scales=ws[:, first + 512 : first + 768],
-                    in_=wg[:, 2048:3072],
-                )
-
-        d_words = d[:].bitcast(F32).rearrange("p j q s u -> p j s u q")
-
-        def b_group(s, engine):
-            if s % 3 == 0:
-                live["gt3", s // 3] = rot.tile([P, 3, 2048], BF16, tag="z", name="gt3", align_bytes=64)
-            gt = live["gt3", s // 3][:, s % 3, :]
-            gt_words = gt.bitcast(F32).rearrange("p (j n u) -> p j n u", j=4, u=2)
-            for jj in range(2):
-                pt = psum.tile([P, 512], F32, tag="t", name="ptt", bufs=4)
-                for jl in range(2):
-                    for u in range(2):
-                        col = 128 * (2 * jl + u)
-                        nc.tensor.transpose(pt[:, col : col + 128], d_words[:, 2 * jj + jl, s, u, :], ident[:])
-                copy_on(
-                    engine,
-                    gt_words[:, 2 * jj : 2 * jj + 2],
-                    pt[:].rearrange("p (j u n) -> p j n u", j=2, u=2),
-                )
-            live["gt", s] = gt
-
-        def b_quant(s):
-            nc.vector.quantize_mx(
-                out=bq[:, 512 * s : 512 * (s + 1)].bitcast(E5M2),
-                scales=bs[:, 512 * s : 512 * (s + 1)],
-                in_=live["gt", s],
-            )
-
-        def out0_tile():
-            o0 = rot.tile([P, 4, 768], F32, tag="z", name="o0", align_bytes=64)
-            live["o0"] = o0
-
-        def out0_open(js):
-            for j in js:
-                pa = psum.tile([P, 512], F32, tag="t", name="pa", bufs=4)
-                pb = psum.tile([P, 512], F32, tag="t", name="pb", bufs=4)
-                live["acc", j] = (pa, pb)
-
-        def out0_place(s, js):
-            for j in js:
-                pa, pb = live["acc", j]
-                col = 512 * s + 128 * j
-                nc.tensor.matmul_mx(
-                    out=pa[:],
-                    lhsT=bq[:, col : col + 128].bitcast(E5M2),
-                    lhsT_scale=bs[:, col : col + 128],
-                    rhs=wq[:, W_BASE[s] : W_BASE[s] + 512].bitcast(E4M3),
-                    rhs_scale=ws[:, W_BASE[s] : W_BASE[s] + 512],
-                    start=(s == 0),
-                    stop=(s == PLACES - 1),
-                )
-                if s >= 2:
-                    nc.tensor.matmul_mx(
-                        out=pb[:],
-                        lhsT=bq[:, col : col + 128].bitcast(E5M2),
-                        lhsT_scale=bs[:, col : col + 128],
-                        rhs=wq[:, W_BASE[s] + 256 : W_BASE[s] + 768].bitcast(E4M3),
-                        rhs_scale=ws[:, W_BASE[s] + 256 : W_BASE[s] + 768],
-                        start=(s == 2),
-                        stop=(s == PLACES - 1),
+        def out1_steps(blk, first_step, count):
+            for step in range(first_step, first_step + count):
+                half, place = divmod(step, PLACES)
+                out1_place(blk, half, place)
+                if place == PLACES - 1:
+                    nc.sync.dma_start(
+                        out=out1_hbm[blk][:, HALF_ROW * half : HALF_ROW * (half + 1)],
+                        in_=stages[(2 * blk + half) % 4][:],
                     )
 
-        def out0_leave(j, engine):
-            o0 = live["o0"]
-            pa, pb = live["acc", j]
-            o0_t = o0[:].rearrange("p j (c h w) -> p j c h w", h=3, w=2)
-            copy_on(engine, o0_t[:, j, :, 0:2, :], pa[:].rearrange("p (h c w) -> p c h w", h=2, w=2))
-            copy_on(engine, o0_t[:, j, :, 2, :], pb[:, 256:512].rearrange("p (c w) -> p c w", w=2))
-            nc.sync.dma_start(out=o0_v[:, j, :], in_=o0[:, j, :])
+        w_taps = w_raw[:].rearrange("p t (c r j) -> p r j c t", r=3 * PLACES, j=3)
 
-        steps = {
-            "ident": lambda: make_identity(nc, ident[:]),
-            "Lx": load_x,
-            "Lz": load_z,
-            "Lg": load_g,
-            "Lw": load_w,
-            "Z0": zero_first,
-            "ZC": zero_copy,
-            "ZK": zero_codes,
-            "XG": x_group,
-            "XQ": x_quant,
-            "M": slope,
-            "T": dz,
-            "GA": a_group,
-            "QA": a_quant,
-            "U": unit,
-            "US": unit_place,
-            "ST": unit_store,
-            "WG": w_group,
-            "WQ": w_quant,
-            "BG": b_group,
-            "BQ": b_quant,
-            "OT": out0_tile,
-            "OO": out0_open,
-            "OP": out0_place,
-            "OE": out0_leave,
-        }
-        for step in SCHEDULE:
-            steps[step[0]](*step[1:])
+        def group_weights(place, half):
+            h, w = divmod(place, 2)
+            first, last = x_rows(h)
+            grouped = rot.tile([P, 3 * 512], BF16, tag="grouped", name="w_grouped", align_bytes=64)
+            for k in range(last - first + 1):
+                nc.vector.tensor_copy(
+                    out=grouped[:, 512 * k : 512 * (k + 1)].rearrange("p (j c t) -> p j c t", j=2, t=PACK),
+                    in_=w_taps[:, 3 * place + first - h + 1 + k, 1 - w : 3 - w, 64 * half : 64 * (half + 1), :],
+                )
+            live["w_grouped", place, half] = grouped
+
+        def quantize_weights(place, half):
+            first, last = x_rows(place // 2)
+            grouped = live["w_grouped", place, half]
+            start = W_WINDOW * (2 * place + half) + 128 * first
+            widths = ((0, 256), (256, 128)) if last - first == 2 else ((0, 256),)
+            for offset, width in widths:
+                nc.vector.quantize_mx(
+                    out=w_codes[:, start + offset : start + offset + width].bitcast(E4M3),
+                    scales=w_scales[:, start + offset : start + offset + width],
+                    in_=grouped[:, PACK * offset : PACK * (offset + width)],
+                )
+
+        dz_words = dz[:].bitcast(F32).rearrange("p slot q s u -> p slot s u q")
+
+        def transpose_dz(place, engine):
+            if place % 3 == 0:
+                live["dzo_grouped", place // 3] = rot.tile(
+                    [P, 3, PACK * 512], BF16, tag="z", name="dzo_grouped", align_bytes=64
+                )
+            grouped = live["dzo_grouped", place // 3][:, place % 3, :]
+            words = grouped.bitcast(F32).rearrange("q (slot p u) -> q slot p u", slot=PACK, u=2)
+            for pair in range(2):
+                turned = psum.tile([P, 512], F32, tag="out0", name="turned")
+                for k in range(2):
+                    for u in range(2):
+                        col = 128 * (2 * k + u)
+                        nc.tensor.transpose(turned[:, col : col + 128], dz_words[:, 2 * pair + k, place, u, :], ident[:])
+                copy_on(
+                    engine,
+                    words[:, 2 * pair : 2 * pair + 2],
+                    turned[:].rearrange("q (slot u p) -> q slot p u", slot=2, u=2),
+                )
+            live["dzo_place", place] = grouped
+
+        def quantize_channels(place):
+            nc.vector.quantize_mx(
+                out=dzo_codes[:, 512 * place : 512 * (place + 1)].bitcast(E5M2),
+                scales=dzo_scales[:, 512 * place : 512 * (place + 1)],
+                in_=live["dzo_place", place],
+            )
+
+        def out0_open(slots):
+            for slot in slots:
+                sum_0 = psum.tile([P, 512], F32, tag="out0", name="sum_0")
+                sum_1 = psum.tile([P, 512], F32, tag="out0", name="sum_1")
+                live["sums", slot] = (sum_0, sum_1)
+
+        def out0_place(place, slots):
+            for slot in slots:
+                col = 512 * place + 128 * slot
+                for half in range(2):
+                    first = W_WINDOW * (2 * place + half)
+                    nc.tensor.matmul_mx(
+                        out=live["sums", slot][half][:],
+                        lhsT=dzo_codes[:, col : col + 128].bitcast(E5M2),
+                        lhsT_scale=dzo_scales[:, col : col + 128],
+                        rhs=w_codes[:, first : first + 512].bitcast(E4M3),
+                        rhs_scale=w_scales[:, first : first + 512],
+                        start=(place == 0),
+                        stop=(place == PLACES - 1),
+                    )
+
+        def out0_leave(slot):
+            rows = live["out0_rows"]
+            for half in range(2):
+                nc.vector.tensor_copy(
+                    out=rows[:, slot, W_WINDOW * half : W_WINDOW * (half + 1)].rearrange("p (c a) -> p c a", a=PLACES),
+                    in_=live["sums", slot][half][:, 0:W_WINDOW].rearrange("p (a c) -> p c a", a=PLACES),
+                )
+            nc.sync.dma_start(out=out0_hbm[:, slot, :], in_=rows[:, slot, :])
+
+        load_x()
+        zero_x_codes()
+        zero_first_stage()
+        load_z(0)
+        load_g(0)
+        load_z(1)
+        load_g(1)
+        group_x()
+        zero_other_stages()
+        make_identity(nc, ident[:])
+        zero_w_codes()
+
+        slope(0)
+        multiply(0)
+        load_z(2)
+        load_g(2)
+        group_samples(0)
+        quantize_x()
+        load_w(0)
+        quantize_samples(0)
+        slope(1)
+        multiply(1)
+        load_z(3)
+        load_g(3)
+        group_samples(1)
+        slope(2)
+        quantize_samples(1)
+        out1_steps(0, 0, 12)
+        load_w(1)
+        multiply(2)
+        slope(3)
+        group_samples(2)
+        multiply(3)
+        quantize_samples(2)
+        out1_steps(1, 0, 12)
+        group_samples(3)
+        group_weights(0, 0)
+        quantize_samples(3)
+
+        for place in range(PLACES):
+            transpose_dz(place, "vector" if place < 4 else "scalar")
+            if place + 1 < PLACES:
+                group_weights(place + 1, 0)
+            quantize_weights(place, 0)
+            out1_steps(2, 2 * place, 2)
+
+        out0_open((0, 1))
+        group_weights(0, 1)
+        for place in range(PLACES):
+            quantize_channels(place)
+            if place + 1 < PLACES:
+                group_weights(place + 1, 1)
+            quantize_weights(place, 1)
+            if place >= 1:
+                out0_place(place - 1, (0, 1))
+            out1_steps(3, 2 * place, 2)
+        out0_place(PLACES - 1, (0, 1))
+
+        live["out0_rows"] = rot.tile([P, PACK, X_ROW], F32, tag="z", name="out0_rows", align_bytes=64)
+        for slot in (0, 1):
+            out0_leave(slot)
+            out0_open((slot + 2,))
+            for place in range(PLACES):
+                out0_place(place, (slot + 2,))
+        out0_leave(2)
+        out0_leave(3)

@@ -20,7 +20,7 @@ ROW = 128 * PLACES * 9
 HALF_ROW = ROW // 2
 CHUNK = 128 * PLACES
 X_ROW = 128 * PLACES
-W_WINDOW = 384
+W_BASE = (0, 512, 1024, 1792, 2560, 3328)
 NEG_SLOPE = 0.1
 
 FLOPS = 2 * 2 * 28 * 512 * 512 * 128
@@ -34,12 +34,12 @@ def x_rows(h):
 def tile_locallyconnected2d_t_v_kernel(tc, x, weight, bias, z, grad_out, out_0, out_1):
     nc = tc.nc
 
-    x_hbm = x.rearrange("(p slot) c h w -> p slot (c h w)", slot=PACK)
+    x_hbm = x.rearrange("(p slot) c xrow xcol -> p slot (c xrow xcol)", slot=PACK)
     z_hbm = z.rearrange("(p slot) o h w -> p slot (o h w)", slot=PACK)
     g_hbm = grad_out.rearrange("(p slot) o h w -> p slot (o h w)", slot=PACK)
-    w_hbm = weight[0].rearrange("(p t) c h w k -> p t (c h w k)", t=PACK)
-    out0_hbm = out_0.rearrange("(p slot) c h w -> p slot (c h w)", slot=PACK)
-    out1_hbm = out_1[0].rearrange("(blk o) c h w k -> blk o (c h w k)", blk=BLOCKS)
+    w_hbm = weight[0].rearrange("(p t) c h w tap -> p t (c h w tap)", t=PACK)
+    out0_hbm = out_0.rearrange("(p slot) c xrow xcol -> p slot (c xrow xcol)", slot=PACK)
+    out1_hbm = out_1[0].rearrange("(blk o) c h w tap -> blk o (c h w tap)", blk=BLOCKS)
 
     def copy_on(engine, out, in_):
         if engine == "scalar":
@@ -54,12 +54,12 @@ def tile_locallyconnected2d_t_v_kernel(tc, x, weight, bias, z, grad_out, out_0, 
         ctx.enter_context(tc.manual_schedule())
 
         ident = keep.tile([P, P], F32, name="ident")
-        x_codes = keep.tile([P, 2 * 512], U32, name="x_codes", align_bytes=64)
-        x_scales = keep.tile([P, 2 * 512], U8, name="x_scales", align_bytes=64)
+        x_codes = keep.tile([P, 4 * 512], U32, name="x_codes", align_bytes=64)
+        x_scales = keep.tile([P, 4 * 512], U8, name="x_scales", align_bytes=64)
         dz = keep.tile([P, PACK, 128, PLACES, PACK], BF16, name="dz", align_bytes=64)
         w_raw = keep.tile([P, PACK, ROW], BF16, name="w_raw", align_bytes=64)
-        w_codes = keep.tile([P, 12 * W_WINDOW + 128], U32, name="w_codes", align_bytes=64)
-        w_scales = keep.tile([P, 12 * W_WINDOW + 128], U8, name="w_scales", align_bytes=64)
+        w_codes = keep.tile([P, 4096], U32, name="w_codes", align_bytes=64)
+        w_scales = keep.tile([P, 4096], U8, name="w_scales", align_bytes=64)
         dzo_codes = keep.tile([P, PLACES * 512], U32, name="dzo_codes", align_bytes=64)
         dzo_scales = keep.tile([P, PLACES * 512], U8, name="dzo_scales", align_bytes=64)
         stage_0 = keep.tile([P, HALF_ROW], F32, name="stage_0", align_bytes=64)
@@ -84,19 +84,15 @@ def tile_locallyconnected2d_t_v_kernel(tc, x, weight, bias, z, grad_out, out_0, 
             nc.sync.dma_start(out=g_sb[:], in_=g_hbm[:, :, CHUNK * blk : CHUNK * (blk + 1)])
             live["g", blk] = g_sb
 
-        def load_w(half):
-            cols = slice(HALF_ROW * half, HALF_ROW * (half + 1))
-            nc.sync.dma_start(out=w_raw[:, :, cols], in_=w_hbm[:, :, cols])
+        def load_w(part):
+            nc.sync.dma_start(out=w_raw[:, 2 * part : 2 * part + 2, :], in_=w_hbm[:, 2 * part : 2 * part + 2, :])
 
-        def zero_x_codes():
+        def zero_codes():
             nc.vector.memset(x_codes[:].bitcast(I32), 0)
             nc.vector.memset(x_scales[:].bitcast(I32), 0)
-
-        def zero_w_codes():
-            starts = [W_WINDOW * v + 256 for v in range(4)] + [W_WINDOW * v for v in range(8, 13)]
-            for first in starts:
-                nc.gpsimd.memset(w_codes[:, first : first + 128].bitcast(F32), 0.0)
-                nc.gpsimd.memset(w_scales[:, first : first + 128], 0)
+            for place in (4, 5):
+                nc.vector.memset(w_codes[:, W_BASE[place] : W_BASE[place] + 256].bitcast(I32), 0)
+                nc.vector.memset(w_scales[:, W_BASE[place] : W_BASE[place] + 256].bitcast(I32), 0)
 
         def zero_first_stage():
             nc.vector.memset(stage_0[:], 0.0)
@@ -106,23 +102,25 @@ def tile_locallyconnected2d_t_v_kernel(tc, x, weight, bias, z, grad_out, out_0, 
                 nc.scalar.copy(out=stage[:], in_=stage_0[:])
 
         def group_x():
-            src = x_raw.rearrange("p slot (c h w) -> p h c w slot", h=3, w=2)
-            for half in range(2):
-                for xrow in range(3):
-                    first = 1536 * half + 512 * xrow
+            src = x_raw.rearrange("p slot (c xrow xcol) -> p xcol xrow c slot", xrow=3, xcol=2)
+            for quarter in range(4):
+                for xcol in range(2):
+                    col0 = 768 * quarter + 384 * xcol
                     nc.vector.tensor_copy(
-                        out=x_grouped[:, first : first + 512].rearrange("p (c w slot) -> p c w slot", w=2, slot=PACK),
-                        in_=src[:, xrow, 64 * half : 64 * (half + 1)],
+                        out=x_grouped[:, col0 : col0 + 384].rearrange(
+                            "p (xrow c slot) -> p xrow c slot", xrow=3, slot=PACK
+                        ),
+                        in_=src[:, xcol, :, 32 * quarter : 32 * (quarter + 1), :],
                     )
 
         def quantize_x():
-            for half in range(2):
-                for first, width in ((0, 256), (256, 128)):
-                    cols = slice(512 * half + first, 512 * half + first + width)
+            for quarter in range(4):
+                for col0, width in ((0, 128), (128, 64)):
+                    cols = slice(512 * quarter + 128 + col0, 512 * quarter + 128 + col0 + width)
                     nc.vector.quantize_mx(
                         out=x_codes[:, cols].bitcast(E4M3),
                         scales=x_scales[:, cols],
-                        in_=x_grouped[:, 1536 * half + PACK * first : 1536 * half + PACK * (first + width)],
+                        in_=x_grouped[:, 768 * quarter + PACK * col0 : 768 * quarter + PACK * (col0 + width)],
                     )
 
         def slope(blk):
@@ -134,16 +132,16 @@ def tile_locallyconnected2d_t_v_kernel(tc, x, weight, bias, z, grad_out, out_0, 
         def multiply(blk):
             nc.vector.tensor_tensor(
                 out=dz[:, :, 32 * blk : 32 * (blk + 1)],
-                in0=live["z", blk][:].rearrange("p slot (q t s) -> p slot q s t", t=PACK, s=PLACES),
-                in1=live["g", blk][:].rearrange("p slot (q t s) -> p slot q s t", t=PACK, s=PLACES),
+                in0=live["z", blk][:].rearrange("p slot (q t place) -> p slot q place t", t=PACK, place=PLACES),
+                in1=live["g", blk][:].rearrange("p slot (q t place) -> p slot q place t", t=PACK, place=PLACES),
                 op=ALU.mult,
             )
 
         def group_samples(blk):
             grouped = rot.tile([P, PACK * CHUNK], BF16, tag="grouped", name="dzn_grouped", align_bytes=64)
             nc.vector.tensor_copy(
-                out=grouped[:].rearrange("p (s q t slot) -> p q s t slot", s=PLACES, t=PACK, slot=PACK),
-                in_=dz[:, :, 32 * blk : 32 * (blk + 1)].rearrange("p slot q s t -> p q s t slot"),
+                out=grouped[:].rearrange("p (place q t slot) -> p q place t slot", place=PLACES, t=PACK, slot=PACK),
+                in_=dz[:, :, 32 * blk : 32 * (blk + 1)].rearrange("p slot q place t -> p q place t slot"),
             )
             live["dzn_grouped", blk] = grouped
 
@@ -151,15 +149,15 @@ def tile_locallyconnected2d_t_v_kernel(tc, x, weight, bias, z, grad_out, out_0, 
             grouped = live["dzn_grouped", blk]
             codes = rot.tile([P, CHUNK], U32, tag="dzn_codes", name="dzn_codes", align_bytes=64)
             scales = rot.tile([P, CHUNK], U8, tag="dzn_scales", name="dzn_scales", align_bytes=64)
-            for first, width in ((0, 512), (512, 256)):
+            for col0, width in ((0, 512), (512, 256)):
                 nc.vector.quantize_mx(
-                    out=codes[:, first : first + width].bitcast(E5M2),
-                    scales=scales[:, first : first + width],
-                    in_=grouped[:, PACK * first : PACK * (first + width)],
+                    out=codes[:, col0 : col0 + width].bitcast(E5M2),
+                    scales=scales[:, col0 : col0 + width],
+                    in_=grouped[:, PACK * col0 : PACK * (col0 + width)],
                 )
             live["dzn", blk] = (codes, scales)
 
-        def out1_place(blk, half, place):
+        def out1_place(blk, quarter, place):
             codes, scales = live["dzn", blk]
             h, w = divmod(place, 2)
             product = psum.tile([P, 512], F32, tag="out1", name="product")
@@ -167,54 +165,62 @@ def tile_locallyconnected2d_t_v_kernel(tc, x, weight, bias, z, grad_out, out_0, 
                 out=product[:],
                 lhsT=codes[:, 128 * place : 128 * (place + 1)].bitcast(E5M2),
                 lhsT_scale=scales[:, 128 * place : 128 * (place + 1)],
-                rhs=x_codes[:, 512 * half : 512 * (half + 1)].bitcast(E4M3),
-                rhs_scale=x_scales[:, 512 * half : 512 * (half + 1)],
+                rhs=x_codes[:, 512 * quarter : 512 * (quarter + 1)].bitcast(E4M3),
+                rhs_scale=x_scales[:, 512 * quarter : 512 * (quarter + 1)],
                 start=True,
                 stop=True,
             )
-            first, last = x_rows(h)
-            stage = stages[(2 * blk + half) % 4][:].rearrange("p (c r j) -> p c r j", r=3 * PLACES, j=3)
+            top, bottom = x_rows(h)
+            c0 = 32 * (quarter % 2)
+            rows = stages[(2 * blk + quarter // 2) % 4][:].rearrange("p (c r j) -> p c r j", r=3 * PLACES, j=3)
             nc.scalar.copy(
-                out=stage[:, :, 3 * place + first - h + 1 : 3 * place + last - h + 2, 1 - w : 3 - w],
-                in_=product[:].rearrange("p (xrow c xcol) -> p c xrow xcol", xrow=4, xcol=2)[:, :, first : last + 1, :],
+                out=rows[:, c0 : c0 + 32, 3 * place + top - h + 1 : 3 * place + bottom - h + 2, :],
+                in_=product[:, 32:416].rearrange("p (plane xrow c) -> p c xrow plane", plane=4, xrow=3)[
+                    :, :, top : bottom + 1, w : w + 3
+                ],
             )
 
-        def out1_steps(blk, first_step, count):
-            for step in range(first_step, first_step + count):
-                half, place = divmod(step, PLACES)
-                out1_place(blk, half, place)
-                if place == PLACES - 1:
-                    nc.sync.dma_start(
-                        out=out1_hbm[blk][:, HALF_ROW * half : HALF_ROW * (half + 1)],
-                        in_=stages[(2 * blk + half) % 4][:],
-                    )
+        def out1_places(blk, half, places):
+            for place in places:
+                out1_place(blk, 2 * half, place)
+                out1_place(blk, 2 * half + 1, place)
 
-        w_taps = w_raw[:].rearrange("p t (c r j) -> p r j c t", r=3 * PLACES, j=3)
+        def out1_store(blk, half):
+            nc.sync.dma_start(
+                out=out1_hbm[blk][:, HALF_ROW * half : HALF_ROW * (half + 1)], in_=stages[(2 * blk + half) % 4][:]
+            )
 
-        def group_weights(place, half):
+        def out1_half(blk, half):
+            out1_places(blk, half, range(PLACES))
+            out1_store(blk, half)
+
+        w_taps = w_raw[:].rearrange("p t (c r j) -> p c r j t", r=3 * PLACES, j=3)
+
+        def group_weights(place):
             h, w = divmod(place, 2)
-            first, last = x_rows(h)
-            grouped = rot.tile([P, 3 * 512], BF16, tag="grouped", name="w_grouped", align_bytes=64)
-            for k in range(last - first + 1):
+            top, bottom = x_rows(h)
+            grouped = rot.tile([P, 3 * 1024], BF16, tag="grouped", name="w_grouped", align_bytes=64)
+            for xrow in range(top, bottom + 1):
+                col0 = 1024 * (xrow - top)
                 nc.vector.tensor_copy(
-                    out=grouped[:, 512 * k : 512 * (k + 1)].rearrange("p (j c t) -> p j c t", j=2, t=PACK),
-                    in_=w_taps[:, 3 * place + first - h + 1 + k, 1 - w : 3 - w, 64 * half : 64 * (half + 1), :],
+                    out=grouped[:, col0 : col0 + 1024].rearrange("p (c xcol t) -> p c xcol t", xcol=2, t=PACK),
+                    in_=w_taps[:, :, 3 * place + xrow - h + 1, 1 - w : 3 - w, :],
                 )
-            live["w_grouped", place, half] = grouped
+            live["w_grouped", place] = grouped
 
-        def quantize_weights(place, half):
-            first, last = x_rows(place // 2)
-            grouped = live["w_grouped", place, half]
-            start = W_WINDOW * (2 * place + half) + 128 * first
-            widths = ((0, 256), (256, 128)) if last - first == 2 else ((0, 256),)
-            for offset, width in widths:
+        def quantize_weights(place):
+            h = place // 2
+            grouped = live["w_grouped", place]
+            base = W_BASE[place] + (256 if h == 2 else 0)
+            widths = ((0, 512), (512, 256)) if h == 1 else ((0, 512),)
+            for col0, width in widths:
                 nc.vector.quantize_mx(
-                    out=w_codes[:, start + offset : start + offset + width].bitcast(E4M3),
-                    scales=w_scales[:, start + offset : start + offset + width],
-                    in_=grouped[:, PACK * offset : PACK * (offset + width)],
+                    out=w_codes[:, base + col0 : base + col0 + width].bitcast(E4M3),
+                    scales=w_scales[:, base + col0 : base + col0 + width],
+                    in_=grouped[:, PACK * col0 : PACK * (col0 + width)],
                 )
 
-        dz_words = dz[:].bitcast(F32).rearrange("p slot q s u -> p slot s u q")
+        dz_words = dz[:].bitcast(F32).rearrange("p slot q place u -> p slot place u q")
 
         def transpose_dz(place, engine):
             if place % 3 == 0:
@@ -225,10 +231,10 @@ def tile_locallyconnected2d_t_v_kernel(tc, x, weight, bias, z, grad_out, out_0, 
             words = grouped.bitcast(F32).rearrange("q (slot p u) -> q slot p u", slot=PACK, u=2)
             for pair in range(2):
                 turned = psum.tile([P, 512], F32, tag="out0", name="turned")
-                for k in range(2):
+                for slot in (2 * pair, 2 * pair + 1):
                     for u in range(2):
-                        col = 128 * (2 * k + u)
-                        nc.tensor.transpose(turned[:, col : col + 128], dz_words[:, 2 * pair + k, place, u, :], ident[:])
+                        col0 = 128 * (2 * (slot % 2) + u)
+                        nc.tensor.transpose(turned[:, col0 : col0 + 128], dz_words[:, slot, place, u, :], ident[:])
                 copy_on(
                     engine,
                     words[:, 2 * pair : 2 * pair + 2],
@@ -245,95 +251,95 @@ def tile_locallyconnected2d_t_v_kernel(tc, x, weight, bias, z, grad_out, out_0, 
 
         def out0_open(slots):
             for slot in slots:
-                sum_0 = psum.tile([P, 512], F32, tag="out0", name="sum_0")
-                sum_1 = psum.tile([P, 512], F32, tag="out0", name="sum_1")
-                live["sums", slot] = (sum_0, sum_1)
+                low = psum.tile([P, 512], F32, tag="out0", name="low")
+                high = psum.tile([P, 512], F32, tag="out0", name="high")
+                live["sums", slot] = (low, high)
 
         def out0_place(place, slots):
             for slot in slots:
-                col = 512 * place + 128 * slot
-                for half in range(2):
-                    first = W_WINDOW * (2 * place + half)
-                    nc.tensor.matmul_mx(
-                        out=live["sums", slot][half][:],
-                        lhsT=dzo_codes[:, col : col + 128].bitcast(E5M2),
-                        lhsT_scale=dzo_scales[:, col : col + 128],
-                        rhs=w_codes[:, first : first + 512].bitcast(E4M3),
-                        rhs_scale=w_scales[:, first : first + 512],
-                        start=(place == 0),
-                        stop=(place == PLACES - 1),
-                    )
+                low, high = live["sums", slot]
+                dz_cols = slice(512 * place + 128 * slot, 512 * place + 128 * (slot + 1))
+                for sums, col0, opens in ((low, W_BASE[place], 0), (high, W_BASE[place] + 256, 2)):
+                    if place >= opens:
+                        nc.tensor.matmul_mx(
+                            out=sums[:],
+                            lhsT=dzo_codes[:, dz_cols].bitcast(E5M2),
+                            lhsT_scale=dzo_scales[:, dz_cols],
+                            rhs=w_codes[:, col0 : col0 + 512].bitcast(E4M3),
+                            rhs_scale=w_scales[:, col0 : col0 + 512],
+                            start=(place == opens),
+                            stop=(place == PLACES - 1),
+                        )
 
         def out0_leave(slot):
-            rows = live["out0_rows"]
-            for half in range(2):
-                nc.vector.tensor_copy(
-                    out=rows[:, slot, W_WINDOW * half : W_WINDOW * (half + 1)].rearrange("p (c a) -> p c a", a=PLACES),
-                    in_=live["sums", slot][half][:, 0:W_WINDOW].rearrange("p (a c) -> p c a", a=PLACES),
-                )
-            nc.sync.dma_start(out=out0_hbm[:, slot, :], in_=rows[:, slot, :])
+            low, high = live["sums", slot]
+            grad_x = live["out0_rows"][:].rearrange("p slot (c xrow xcol) -> p slot c xrow xcol", xrow=3, xcol=2)
+            nc.vector.tensor_copy(
+                out=grad_x[:, slot, :, 0:2, :],
+                in_=low[:].rearrange("p (xrow c xcol) -> p c xrow xcol", xrow=2, xcol=2),
+            )
+            nc.vector.tensor_copy(
+                out=grad_x[:, slot, :, 2, :], in_=high[:, 256:512].rearrange("p (c xcol) -> p c xcol", xcol=2)
+            )
+            nc.sync.dma_start(out=out0_hbm[:, slot, :], in_=live["out0_rows"][:, slot, :])
 
+        make_identity(nc, ident[:])
         load_x()
-        zero_x_codes()
-        zero_first_stage()
         load_z(0)
         load_g(0)
         load_z(1)
         load_g(1)
-        group_x()
+        zero_first_stage()
+        zero_codes()
         zero_other_stages()
-        make_identity(nc, ident[:])
-        zero_w_codes()
-
-        slope(0)
-        multiply(0)
-        load_z(2)
-        load_g(2)
-        group_samples(0)
+        group_x()
         quantize_x()
-        load_w(0)
-        quantize_samples(0)
-        slope(1)
-        multiply(1)
-        load_z(3)
-        load_g(3)
-        group_samples(1)
-        slope(2)
-        quantize_samples(1)
-        out1_steps(0, 0, 12)
-        load_w(1)
-        multiply(2)
-        slope(3)
-        group_samples(2)
-        multiply(3)
-        quantize_samples(2)
-        out1_steps(1, 0, 12)
-        group_samples(3)
-        group_weights(0, 0)
-        quantize_samples(3)
 
-        for place in range(PLACES):
-            transpose_dz(place, "vector" if place < 4 else "scalar")
-            if place + 1 < PLACES:
-                group_weights(place + 1, 0)
-            quantize_weights(place, 0)
-            out1_steps(2, 2 * place, 2)
+        for blk in range(BLOCKS):
+            slope(blk)
+            multiply(blk)
+            if blk + 2 < BLOCKS:
+                load_z(blk + 2)
+                load_g(blk + 2)
+            if blk == 0:
+                load_w(0)
+            group_samples(blk)
+            quantize_samples(blk)
+            if blk == 1:
+                out1_half(0, 0)
+                load_w(1)
+                out1_half(0, 1)
+            if blk == 2:
+                out1_half(1, 0)
+                out1_half(1, 1)
+
+        for place in range(3):
+            transpose_dz(place, "vector")
+            transpose_dz(place + 3, "scalar")
+            if place >= 1:
+                quantize_channels(place - 1)
+        quantize_channels(2)
+        out1_half(2, 0)
 
         out0_open((0, 1))
-        group_weights(0, 1)
+        group_weights(0)
         for place in range(PLACES):
-            quantize_channels(place)
+            if 2 <= place <= 4:
+                quantize_channels(place + 1)
             if place + 1 < PLACES:
-                group_weights(place + 1, 1)
-            quantize_weights(place, 1)
-            if place >= 1:
-                out0_place(place - 1, (0, 1))
-            out1_steps(3, 2 * place, 2)
-        out0_place(PLACES - 1, (0, 1))
+                group_weights(place + 1)
+            quantize_weights(place)
+            out0_place(place, (0, 1))
+            blk, half = ((2, 1), (3, 0), (3, 1))[place // 2]
+            out1_places(blk, half, range(3 * (place % 2), 3 * (place % 2) + 3))
+            if place in (1, 3):
+                out1_store(blk, half)
 
         live["out0_rows"] = rot.tile([P, PACK, X_ROW], F32, tag="z", name="out0_rows", align_bytes=64)
         for slot in (0, 1):
             out0_leave(slot)
+            if slot == 1:
+                out1_store(3, 1)
             out0_open((slot + 2,))
             for place in range(PLACES):
                 out0_place(place, (slot + 2,))

@@ -54,9 +54,9 @@ def tile_locallyconnected2d_t_v_kernel(tc, x, weight, bias, z, grad_out, out_0, 
         ctx.enter_context(tc.manual_schedule())
 
         ident = keep.tile([P, P], F32, name="ident")
-        x_codes = keep.tile([P, 4 * 512], U32, name="x_codes", align_bytes=64)
-        x_scales = keep.tile([P, 4 * 512], U8, name="x_scales", align_bytes=64)
-        dz = keep.tile([P, PACK, 128, PLACES, PACK], BF16, name="dz", align_bytes=64)
+        x_codes = keep.tile([P, 2 * 512], U32, name="x_codes", align_bytes=64)
+        x_scales = keep.tile([P, 2 * 512], U8, name="x_scales", align_bytes=64)
+        dz_words = keep.tile([P, PACK, PLACES, 2, 128], F32, name="dz_words", align_bytes=64)
         w_raw = keep.tile([P, PACK, ROW], BF16, name="w_raw", align_bytes=64)
         w_codes = keep.tile([P, 4096], U32, name="w_codes", align_bytes=64)
         w_scales = keep.tile([P, 4096], U8, name="w_scales", align_bytes=64)
@@ -88,8 +88,9 @@ def tile_locallyconnected2d_t_v_kernel(tc, x, weight, bias, z, grad_out, out_0, 
             nc.sync.dma_start(out=w_raw[:, 2 * part : 2 * part + 2, :], in_=w_hbm[:, 2 * part : 2 * part + 2, :])
 
         def zero_codes():
-            nc.vector.memset(x_codes[:].bitcast(I32), 0)
-            nc.vector.memset(x_scales[:].bitcast(I32), 0)
+            for half in range(2):
+                nc.vector.memset(x_codes[:, 512 * half + 384 : 512 * (half + 1)].bitcast(I32), 0)
+                nc.vector.memset(x_scales[:, 512 * half + 384 : 512 * (half + 1)].bitcast(I32), 0)
             for place in (4, 5):
                 nc.vector.memset(w_codes[:, W_BASE[place] : W_BASE[place] + 256].bitcast(I32), 0)
                 nc.vector.memset(w_scales[:, W_BASE[place] : W_BASE[place] + 256].bitcast(I32), 0)
@@ -102,25 +103,25 @@ def tile_locallyconnected2d_t_v_kernel(tc, x, weight, bias, z, grad_out, out_0, 
                 nc.scalar.copy(out=stage[:], in_=stage_0[:])
 
         def group_x():
-            src = x_raw.rearrange("p slot (c xrow xcol) -> p xcol xrow c slot", xrow=3, xcol=2)
-            for quarter in range(4):
-                for xcol in range(2):
-                    col0 = 768 * quarter + 384 * xcol
+            src = x_raw.rearrange("p slot (c xrow xcol) -> p xrow c xcol slot", xrow=3, xcol=2)
+            for half in range(2):
+                for xrow in range(3):
+                    col0 = 1536 * half + 512 * xrow
                     nc.vector.tensor_copy(
-                        out=x_grouped[:, col0 : col0 + 384].rearrange(
-                            "p (xrow c slot) -> p xrow c slot", xrow=3, slot=PACK
+                        out=x_grouped[:, col0 : col0 + 512].rearrange(
+                            "p (c xcol slot) -> p c xcol slot", xcol=2, slot=PACK
                         ),
-                        in_=src[:, xcol, :, 32 * quarter : 32 * (quarter + 1), :],
+                        in_=src[:, xrow, 64 * half : 64 * (half + 1)],
                     )
 
         def quantize_x():
-            for quarter in range(4):
-                for col0, width in ((0, 128), (128, 64)):
-                    cols = slice(512 * quarter + 128 + col0, 512 * quarter + 128 + col0 + width)
+            for half in range(2):
+                for col0, width in ((0, 256), (256, 128)):
+                    cols = slice(512 * half + col0, 512 * half + col0 + width)
                     nc.vector.quantize_mx(
                         out=x_codes[:, cols].bitcast(E4M3),
                         scales=x_scales[:, cols],
-                        in_=x_grouped[:, 768 * quarter + PACK * col0 : 768 * quarter + PACK * (col0 + width)],
+                        in_=x_grouped[:, 1536 * half + PACK * col0 : 1536 * half + PACK * (col0 + width)],
                     )
 
         def slope(blk):
@@ -130,18 +131,26 @@ def tile_locallyconnected2d_t_v_kernel(tc, x, weight, bias, z, grad_out, out_0, 
             )
 
         def multiply(blk):
+            dz_blk = rot.tile([P, PACK, 32, PLACES, PACK], BF16, tag="dz_blk", name="dz_blk", bufs=1, align_bytes=64)
             nc.vector.tensor_tensor(
-                out=dz[:, :, 32 * blk : 32 * (blk + 1)],
+                out=dz_blk[:],
                 in0=live["z", blk][:].rearrange("p slot (q t place) -> p slot q place t", t=PACK, place=PLACES),
                 in1=live["g", blk][:].rearrange("p slot (q t place) -> p slot q place t", t=PACK, place=PLACES),
                 op=ALU.mult,
+            )
+            live["dz_blk", blk] = dz_blk
+
+        def sort_words(blk):
+            nc.vector.tensor_copy(
+                out=dz_words[:, :, :, :, 32 * blk : 32 * (blk + 1)],
+                in_=live["dz_blk", blk][:].bitcast(F32).rearrange("p slot q place u -> p slot place u q"),
             )
 
         def group_samples(blk):
             grouped = rot.tile([P, PACK * CHUNK], BF16, tag="grouped", name="dzn_grouped", align_bytes=64)
             nc.vector.tensor_copy(
                 out=grouped[:].rearrange("p (place q t slot) -> p q place t slot", place=PLACES, t=PACK, slot=PACK),
-                in_=dz[:, :, 32 * blk : 32 * (blk + 1)].rearrange("p slot q place t -> p q place t slot"),
+                in_=live["dz_blk", blk][:].rearrange("p slot q place t -> p q place t slot"),
             )
             live["dzn_grouped", blk] = grouped
 
@@ -157,7 +166,7 @@ def tile_locallyconnected2d_t_v_kernel(tc, x, weight, bias, z, grad_out, out_0, 
                 )
             live["dzn", blk] = (codes, scales)
 
-        def out1_place(blk, quarter, place):
+        def out1_place(blk, half, place):
             codes, scales = live["dzn", blk]
             h, w = divmod(place, 2)
             product = psum.tile([P, 512], F32, tag="out1", name="product")
@@ -165,25 +174,21 @@ def tile_locallyconnected2d_t_v_kernel(tc, x, weight, bias, z, grad_out, out_0, 
                 out=product[:],
                 lhsT=codes[:, 128 * place : 128 * (place + 1)].bitcast(E5M2),
                 lhsT_scale=scales[:, 128 * place : 128 * (place + 1)],
-                rhs=x_codes[:, 512 * quarter : 512 * (quarter + 1)].bitcast(E4M3),
-                rhs_scale=x_scales[:, 512 * quarter : 512 * (quarter + 1)],
+                rhs=x_codes[:, 512 * half : 512 * (half + 1)].bitcast(E4M3),
+                rhs_scale=x_scales[:, 512 * half : 512 * (half + 1)],
                 start=True,
                 stop=True,
             )
             top, bottom = x_rows(h)
-            c0 = 32 * (quarter % 2)
-            rows = stages[(2 * blk + quarter // 2) % 4][:].rearrange("p (c r j) -> p c r j", r=3 * PLACES, j=3)
+            rows = stages[(2 * blk + half) % 4][:].rearrange("p (c r j) -> p c r j", r=3 * PLACES, j=3)
             nc.scalar.copy(
-                out=rows[:, c0 : c0 + 32, 3 * place + top - h + 1 : 3 * place + bottom - h + 2, :],
-                in_=product[:, 32:416].rearrange("p (plane xrow c) -> p c xrow plane", plane=4, xrow=3)[
-                    :, :, top : bottom + 1, w : w + 3
-                ],
+                out=rows[:, :, 3 * place + top - h + 1 : 3 * place + bottom - h + 2, 1 - w : 3 - w],
+                in_=product[:].rearrange("p (xrow c xcol) -> p c xrow xcol", xrow=4, xcol=2)[:, :, top : bottom + 1, :],
             )
 
         def out1_places(blk, half, places):
             for place in places:
-                out1_place(blk, 2 * half, place)
-                out1_place(blk, 2 * half + 1, place)
+                out1_place(blk, half, place)
 
         def out1_store(blk, half):
             nc.sync.dma_start(
@@ -219,8 +224,6 @@ def tile_locallyconnected2d_t_v_kernel(tc, x, weight, bias, z, grad_out, out_0, 
                     scales=w_scales[:, base + col0 : base + col0 + width],
                     in_=grouped[:, PACK * col0 : PACK * (col0 + width)],
                 )
-
-        dz_words = dz[:].bitcast(F32).rearrange("p slot q place u -> p slot place u q")
 
         def transpose_dz(place, engine):
             if place % 3 == 0:
@@ -304,6 +307,7 @@ def tile_locallyconnected2d_t_v_kernel(tc, x, weight, bias, z, grad_out, out_0, 
             if blk == 0:
                 load_w(0)
             group_samples(blk)
+            sort_words(blk)
             quantize_samples(blk)
             if blk == 1:
                 out1_half(0, 0)

from contextlib import ExitStack

import concourse.mybir as mybir
from concourse.masks import make_identity

F32 = mybir.dt.float32
BF16 = mybir.dt.bfloat16
U32 = mybir.dt.uint32
U8 = mybir.dt.uint8
I32 = mybir.dt.int32
E4M3 = mybir.dt.float8_e4m3fn_x4
E5M2 = mybir.dt.float8_e5m2_x4
ALU = mybir.AluOpType

P = 128
PACK = 4
PLACES = 6
BLOCKS = 4
ROW = 128 * PLACES * 9
HALF_ROW = ROW // 2
CHUNK = 128 * PLACES
X_ROW = 128 * PLACES
W_BASE = (0, 512, 1024, 1792, 2560, 3328)
NEG_SLOPE = 0.1

FLOPS = 2 * 2 * 28 * 512 * 512 * 128
BYTES = 2 * 512 * X_ROW + 2 * 28 * 512 * 128 + (4 + 2) * 512 * 512 * PLACES + 4 * 512 * X_ROW + 4 * 512 * ROW


def x_rows(h):
    return max(0, h - 1), min(2, h + 1)


def tile_locallyconnected2d_t_v_kernel(tc, x, weight, bias, z, grad_out, out_0, out_1):
    nc = tc.nc

    x_hbm = x.rearrange("(p slot) c xrow xcol -> p slot (c xrow xcol)", slot=PACK)
    z_hbm = z.rearrange("(p slot) o h w -> p slot (o h w)", slot=PACK)
    g_hbm = grad_out.rearrange("(p slot) o h w -> p slot (o h w)", slot=PACK)
    w_hbm = weight[0].rearrange("(p t) c h w tap -> p t (c h w tap)", t=PACK)
    out0_hbm = out_0.rearrange("(p slot) c xrow xcol -> p slot (c xrow xcol)", slot=PACK)
    out1_hbm = out_1[0].rearrange("(blk o) c h w tap -> blk o (c h w tap)", blk=BLOCKS)

    def copy_on(engine, out, in_):
        if engine == "scalar":
            nc.scalar.copy(out=out, in_=in_)
        else:
            nc.vector.tensor_copy(out=out, in_=in_)

    with ExitStack() as ctx:
        keep = ctx.enter_context(tc.tile_pool(name="keep", bufs=1))
        rot = ctx.enter_context(tc.tile_pool(name="rot", bufs=2))
        psum = ctx.enter_context(tc.psum_pool(name="psum", bufs=4))
        ctx.enter_context(tc.manual_schedule())

        ident = keep.tile([P, P], F32, name="ident")
        x_codes = keep.tile([P, 2 * 512], U32, name="x_codes", align_bytes=64)
        x_scales = keep.tile([P, 2 * 512], U8, name="x_scales", align_bytes=64)
        dz_words = keep.tile([P, PACK, PLACES, 2, 128], F32, name="dz_words", align_bytes=64)
        w_raw = keep.tile([P, PACK, ROW], BF16, name="w_raw", align_bytes=64)
        w_codes = keep.tile([P, 4096], U32, name="w_codes", align_bytes=64)
        w_scales = keep.tile([P, 4096], U8, name="w_scales", align_bytes=64)
        dzo_codes = keep.tile([P, PLACES * 512], U32, name="dzo_codes", align_bytes=64)
        dzo_scales = keep.tile([P, PLACES * 512], U8, name="dzo_scales", align_bytes=64)
        stage_0 = keep.tile([P, HALF_ROW], F32, name="stage_0", align_bytes=64)
        stage_1 = keep.tile([P, HALF_ROW], F32, name="stage_1", align_bytes=64)
        stage_2 = keep.tile([P, HALF_ROW], F32, name="stage_2", align_bytes=64)
        stage_3 = keep.tile([P, HALF_ROW], F32, name="stage_3", align_bytes=64)
        stages = (stage_0, stage_1, stage_2, stage_3)
        x_raw = w_raw[:, 3, 0:3072].rearrange("p (slot f) -> p slot f", slot=PACK)
        x_grouped = w_raw[:, 3, 3072:6144]
        live = {}

        def load_x():
            nc.sync.dma_start(out=x_raw, in_=x_hbm)

        def load_z(blk):
            z_sb = rot.tile([P, PACK, CHUNK], F32, tag="z", name="z_sb", align_bytes=64)
            nc.sync.dma_start(out=z_sb[:], in_=z_hbm[:, :, CHUNK * blk : CHUNK * (blk + 1)])
            live["z", blk] = z_sb

        def load_g(blk):
            g_sb = rot.tile([P, PACK, CHUNK], BF16, tag="g", name="g_sb", align_bytes=64)
            nc.sync.dma_start(out=g_sb[:], in_=g_hbm[:, :, CHUNK * blk : CHUNK * (blk + 1)])
            live["g", blk] = g_sb

        def load_w(part):
            nc.sync.dma_start(out=w_raw[:, 2 * part : 2 * part + 2, :], in_=w_hbm[:, 2 * part : 2 * part + 2, :])

        def zero_codes():
            for half in range(2):
                nc.vector.memset(x_codes[:, 512 * half + 384 : 512 * (half + 1)].bitcast(I32), 0)
                nc.vector.memset(x_scales[:, 512 * half + 384 : 512 * (half + 1)].bitcast(I32), 0)
            for place in (4, 5):
                nc.vector.memset(w_codes[:, W_BASE[place] : W_BASE[place] + 256].bitcast(I32), 0)
                nc.vector.memset(w_scales[:, W_BASE[place] : W_BASE[place] + 256].bitcast(I32), 0)

        def zero_first_stage():
            nc.vector.memset(stage_0[:], 0.0)

        def zero_other_stages():
            for stage in stages[1:]:
                nc.scalar.copy(out=stage[:], in_=stage_0[:])

        def group_x():
            src = x_raw.rearrange("p slot (c xrow xcol) -> p xrow c xcol slot", xrow=3, xcol=2)
            for half in range(2):
                for xrow in range(3):
                    col0 = 1536 * half + 512 * xrow
                    nc.vector.tensor_copy(
                        out=x_grouped[:, col0 : col0 + 512].rearrange(
                            "p (c xcol slot) -> p c xcol slot", xcol=2, slot=PACK
                        ),
                        in_=src[:, xrow, 64 * half : 64 * (half + 1)],
                    )

        def quantize_x():
            for half in range(2):
                for col0, width in ((0, 256), (256, 128)):
                    cols = slice(512 * half + col0, 512 * half + col0 + width)
                    nc.vector.quantize_mx(
                        out=x_codes[:, cols].bitcast(E4M3),
                        scales=x_scales[:, cols],
                        in_=x_grouped[:, 1536 * half + PACK * col0 : 1536 * half + PACK * (col0 + width)],
                    )

        def slope(blk):
            z_sb = live["z", blk]
            nc.vector.tensor_scalar(
                out=z_sb[:], in0=z_sb[:], scalar1=0.0, scalar2=NEG_SLOPE, op0=ALU.is_ge, op1=ALU.max
            )

        def multiply(blk):
            dz_blk = rot.tile([P, PACK, 32, PLACES, PACK], BF16, tag="dz_blk", name="dz_blk", bufs=1, align_bytes=64)
            nc.vector.tensor_tensor(
                out=dz_blk[:],
                in0=live["z", blk][:].rearrange("p slot (q t place) -> p slot q place t", t=PACK, place=PLACES),
                in1=live["g", blk][:].rearrange("p slot (q t place) -> p slot q place t", t=PACK, place=PLACES),
                op=ALU.mult,
            )
            live["dz_blk", blk] = dz_blk

        def sort_words(blk):
            nc.vector.tensor_copy(
                out=dz_words[:, :, :, :, 32 * blk : 32 * (blk + 1)],
                in_=live["dz_blk", blk][:].bitcast(F32).rearrange("p slot q place u -> p slot place u q"),
            )

        def group_samples(blk):
            grouped = rot.tile([P, PACK * CHUNK], BF16, tag="grouped", name="dzn_grouped", align_bytes=64)
            nc.vector.tensor_copy(
                out=grouped[:].rearrange("p (place q t slot) -> p q place t slot", place=PLACES, t=PACK, slot=PACK),
                in_=live["dz_blk", blk][:].rearrange("p slot q place t -> p q place t slot"),
            )
            live["dzn_grouped", blk] = grouped

        def quantize_samples(blk):
            grouped = live["dzn_grouped", blk]
            codes = rot.tile([P, CHUNK], U32, tag="dzn_codes", name="dzn_codes", align_bytes=64)
            scales = rot.tile([P, CHUNK], U8, tag="dzn_scales", name="dzn_scales", align_bytes=64)
            for col0, width in ((0, 512), (512, 256)):
                nc.vector.quantize_mx(
                    out=codes[:, col0 : col0 + width].bitcast(E5M2),
                    scales=scales[:, col0 : col0 + width],
                    in_=grouped[:, PACK * col0 : PACK * (col0 + width)],
                )
            live["dzn", blk] = (codes, scales)

        def out1_place(blk, half, place):
            codes, scales = live["dzn", blk]
            h, w = divmod(place, 2)
            product = psum.tile([P, 512], F32, tag="out1", name="product")
            nc.tensor.matmul_mx(
                out=product[:],
                lhsT=codes[:, 128 * place : 128 * (place + 1)].bitcast(E5M2),
                lhsT_scale=scales[:, 128 * place : 128 * (place + 1)],
                rhs=x_codes[:, 512 * half : 512 * (half + 1)].bitcast(E4M3),
                rhs_scale=x_scales[:, 512 * half : 512 * (half + 1)],
                start=True,
                stop=True,
            )
            top, bottom = x_rows(h)
            rows = stages[(2 * blk + half) % 4][:].rearrange("p (c r j) -> p c r j", r=3 * PLACES, j=3)
            nc.scalar.copy(
                out=rows[:, :, 3 * place + top - h + 1 : 3 * place + bottom - h + 2, 1 - w : 3 - w],
                in_=product[:].rearrange("p (xrow c xcol) -> p c xrow xcol", xrow=4, xcol=2)[:, :, top : bottom + 1, :],
            )

        def out1_places(blk, half, places):
            for place in places:
                out1_place(blk, half, place)

        def out1_store(blk, half):
            nc.sync.dma_start(
                out=out1_hbm[blk][:, HALF_ROW * half : HALF_ROW * (half + 1)], in_=stages[(2 * blk + half) % 4][:]
            )

        def out1_half(blk, half):
            out1_places(blk, half, range(PLACES))
            out1_store(blk, half)

        w_taps = w_raw[:].rearrange("p t (c r j) -> p c r j t", r=3 * PLACES, j=3)

        def group_weights(place):
            h, w = divmod(place, 2)
            top, bottom = x_rows(h)
            grouped = rot.tile([P, 3 * 1024], BF16, tag="grouped", name="w_grouped", align_bytes=64)
            for xrow in range(top, bottom + 1):
                col0 = 1024 * (xrow - top)
                nc.vector.tensor_copy(
                    out=grouped[:, col0 : col0 + 1024].rearrange("p (c xcol t) -> p c xcol t", xcol=2, t=PACK),
                    in_=w_taps[:, :, 3 * place + xrow - h + 1, 1 - w : 3 - w, :],
                )
            live["w_grouped", place] = grouped

        def quantize_weights(place):
            h = place // 2
            grouped = live["w_grouped", place]
            base = W_BASE[place] + (256 if h == 2 else 0)
            widths = ((0, 512), (512, 256)) if h == 1 else ((0, 512),)
            for col0, width in widths:
                nc.vector.quantize_mx(
                    out=w_codes[:, base + col0 : base + col0 + width].bitcast(E4M3),
                    scales=w_scales[:, base + col0 : base + col0 + width],
                    in_=grouped[:, PACK * col0 : PACK * (col0 + width)],
                )

        def transpose_dz(place, engine):
            if place % 3 == 0:
                live["dzo_grouped", place // 3] = rot.tile(
                    [P, 3, PACK * 512], BF16, tag="z", name="dzo_grouped", align_bytes=64
                )
            grouped = live["dzo_grouped", place // 3][:, place % 3, :]
            words = grouped.bitcast(F32).rearrange("q (slot p u) -> q slot p u", slot=PACK, u=2)
            for pair in range(2):
                turned = psum.tile([P, 512], F32, tag="out0", name="turned")
                for slot in (2 * pair, 2 * pair + 1):
                    for u in range(2):
                        col0 = 128 * (2 * (slot % 2) + u)
                        nc.tensor.transpose(turned[:, col0 : col0 + 128], dz_words[:, slot, place, u, :], ident[:])
                copy_on(
                    engine,
                    words[:, 2 * pair : 2 * pair + 2],
                    turned[:].rearrange("q (slot u p) -> q slot p u", slot=2, u=2),
                )
            live["dzo_place", place] = grouped

        def quantize_channels(place):
            nc.vector.quantize_mx(
                out=dzo_codes[:, 512 * place : 512 * (place + 1)].bitcast(E5M2),
                scales=dzo_scales[:, 512 * place : 512 * (place + 1)],
                in_=live["dzo_place", place],
            )

        def out0_open(slots):
            for slot in slots:
                low = psum.tile([P, 512], F32, tag="out0", name="low")
                high = psum.tile([P, 512], F32, tag="out0", name="high")
                live["sums", slot] = (low, high)

        def out0_place(place, slots):
            for slot in slots:
                low, high = live["sums", slot]
                dz_cols = slice(512 * place + 128 * slot, 512 * place + 128 * (slot + 1))
                for sums, col0, opens in ((low, W_BASE[place], 0), (high, W_BASE[place] + 256, 2)):
                    if place >= opens:
                        nc.tensor.matmul_mx(
                            out=sums[:],
                            lhsT=dzo_codes[:, dz_cols].bitcast(E5M2),
                            lhsT_scale=dzo_scales[:, dz_cols],
                            rhs=w_codes[:, col0 : col0 + 512].bitcast(E4M3),
                            rhs_scale=w_scales[:, col0 : col0 + 512],
                            start=(place == opens),
                            stop=(place == PLACES - 1),
                        )

        def out0_leave(slot):
            low, high = live["sums", slot]
            grad_x = live["out0_rows"][:].rearrange("p slot (c xrow xcol) -> p slot c xrow xcol", xrow=3, xcol=2)
            nc.vector.tensor_copy(
                out=grad_x[:, slot, :, 0:2, :],
                in_=low[:].rearrange("p (xrow c xcol) -> p c xrow xcol", xrow=2, xcol=2),
            )
            nc.vector.tensor_copy(
                out=grad_x[:, slot, :, 2, :], in_=high[:, 256:512].rearrange("p (c xcol) -> p c xcol", xcol=2)
            )
            nc.sync.dma_start(out=out0_hbm[:, slot, :], in_=live["out0_rows"][:, slot, :])

        make_identity(nc, ident[:])
        load_x()
        load_z(0)
        load_g(0)
        load_z(1)
        load_g(1)
        zero_first_stage()
        zero_codes()
        zero_other_stages()
        group_x()
        quantize_x()

        for blk in range(BLOCKS):
            slope(blk)
            multiply(blk)
            if blk + 2 < BLOCKS:
                load_z(blk + 2)
                load_g(blk + 2)
            if blk == 0:
                load_w(0)
            group_samples(blk)
            sort_words(blk)
            quantize_samples(blk)
            if blk == 1:
                out1_half(0, 0)
                load_w(1)
                out1_half(0, 1)
            if blk == 2:
                out1_half(1, 0)
                out1_half(1, 1)

        for place in range(3):
            transpose_dz(place, "vector")
            transpose_dz(place + 3, "scalar")
            if place >= 1:
                quantize_channels(place - 1)
        quantize_channels(2)
        out1_half(2, 0)

        out0_open((0, 1))
        group_weights(0)
        for place in range(PLACES):
            if 2 <= place <= 4:
                quantize_channels(place + 1)
            if place + 1 < PLACES:
                group_weights(place + 1)
            quantize_weights(place)
            out0_place(place, (0, 1))
            blk, half = ((2, 1), (3, 0), (3, 1))[place // 2]
            out1_places(blk, half, range(3 * (place % 2), 3 * (place % 2) + 3))
            if place in (1, 3):
                out1_store(blk, half)

        live["out0_rows"] = rot.tile([P, PACK, X_ROW], F32, tag="z", name="out0_rows", align_bytes=64)
        for slot in (0, 1):
            out0_leave(slot)
            if slot == 1:
                out1_store(3, 1)
            out0_open((slot + 2,))
            for place in range(PLACES):
                out0_place(place, (slot + 2,))
        out0_leave(2)
        out0_leave(3)
